import numpy as np
import ml_dtypes


def mxq(x, axis, fmt="e4m3"):
    dtype, down = {"e4m3": (ml_dtypes.float8_e4m3fn, 7), "e5m2": (ml_dtypes.float8_e5m2, 14)}[fmt]
    v = np.moveaxis(np.asarray(x, np.float32).astype(ml_dtypes.bfloat16).astype(np.float64), axis, -1)
    blocks = v.reshape(v.shape[:-1] + (-1, 32))
    amax = np.abs(blocks).max(-1, keepdims=True)
    byte = np.maximum(np.where(amax > 0, np.frexp(amax)[1] - 1 + 127, 0) - down, 1)
    scale = np.exp2(byte - 127.0)
    codes = (blocks / scale).astype(np.float32).astype(dtype).astype(np.float64)
    return np.moveaxis((codes * scale).reshape(v.shape), -1, axis)


WIDE = False


def mx_kscale(k):
    if not WIDE:
        return np.ones(k)
    levels = np.array([10, -10, 5, -5, 0])
    a = np.random.permutation(np.resize(levels, k // 512 * 4)).reshape(k // 512, 4)
    idx = np.arange(k)
    return np.exp2(a[idx // 512, idx % 128 // 32])


BF16 = ml_dtypes.bfloat16


def bf(x):
    return np.asarray(x, np.float32).astype(BF16)


def f64(x):
    return np.asarray(x).astype(np.float64)


R, C, E, H = 32, 256, 512, 8
D = E // H
RD = R * D


def setup_inputs():
    s = mx_kscale(E)
    t = mx_kscale(E)
    g = 1.5 / np.sqrt(E)
    return {"x": bf(np.random.standard_normal((R, C, E)) * s),
            "mask": bf(np.random.uniform(size=(R, C)) < 0.1),
            "Wq": bf(np.random.standard_normal((E, E)) * g / s[:, None] * t),
            "bq": bf(np.random.standard_normal(E) * 0.1 * t),
            "Wk": bf(np.random.standard_normal((E, E)) * g / s[:, None] / t),
            "bk": bf(np.random.standard_normal(E) * 0.1 / t)}


def reference(x, mask, Wq, bq, Wk, bk):
    scaling = (D ** -0.5) / np.sqrt(R)
    xq = mxq(f64(x), 2, "e4m3")
    q = ((xq @ mxq(f64(Wq), 0, "e4m3")) + f64(bq)).reshape(R, C, H, D)
    k = ((xq @ mxq(f64(Wk), 0, "e4m3")) + f64(bk)).reshape(R, C, H, D)
    q = q * scaling
    q = q * (1.0 - f64(mask)[:, :, None, None])
    qm = q.transpose(2, 1, 0, 3).reshape(H, C, RD)
    km = k.transpose(2, 1, 0, 3).reshape(H, C, RD)
    return mxq(qm, 2, "e4m3") @ mxq(km, 2, "e4m3").transpose(0, 2, 1)

@@ -1,0 +1,227 @@
+from contextlib import ExitStack
+
+import concourse.mybir as mybir
+from concourse.masks import make_identity
+
+F32 = mybir.dt.float32
+BF16 = mybir.dt.bfloat16
+U32 = mybir.dt.uint32
+I32 = mybir.dt.int32
+U8 = mybir.dt.uint8
+FP8X4 = mybir.dt.float8_e4m3fn_x4
+ADD = mybir.AluOpType.add
+MULT = mybir.AluOpType.mult
+ACT = mybir.ActivationFunctionType
+
+ROWS, COLS, EMBED, HEADS = 32, 256, 512, 8
+HEAD_DIM = EMBED // HEADS
+SCALING = HEAD_DIM**-0.5 / ROWS**0.5
+
+P = 128
+PACK = 4
+ROW_GROUPS = ROWS // PACK
+COL_HALVES = COLS // P
+FEATURE_TILES = EMBED // P
+HALF = P // 2
+TOKENS = P * PACK
+STREAMED_TILES = 2
+CODE_SETS = 3
+SPLIT = 4
+
+FLOPS = 2 * ROWS * COLS * EMBED * 2 * EMBED + 2 * HEADS * COLS * COLS * ROWS * HEAD_DIM
+
+
+def tile_rowselfattention_pa_t_kernel(tc, x, mask, Wq, bq, Wk, bk, out):
+    nc = tc.nc
+    with ExitStack() as stack:
+        const = stack.enter_context(tc.tile_pool(name="const", bufs=1))
+        weights = stack.enter_context(tc.tile_pool(name="weights", bufs=2))
+        x_pool = stack.enter_context(tc.tile_pool(name="x_pool", bufs=4))
+        grouped_pool = stack.enter_context(tc.tile_pool(name="grouped_pool", bufs=3))
+        qk_pool = stack.enter_context(tc.tile_pool(name="qk_pool", bufs=3))
+        out_pool = stack.enter_context(tc.tile_pool(name="out_pool", bufs=2))
+        work = stack.enter_context(tc.psum_pool(name="work", bufs=6))
+        logit_banks = stack.enter_context(tc.psum_pool(name="logit_banks", bufs=2))
+
+        ident_f32 = const.tile([P, P], F32)
+        make_identity(nc, ident_f32[:])
+        ident_bf = const.tile([P, P], BF16)
+        nc.vector.tensor_copy(out=ident_bf[:], in_=ident_f32[:])
+
+        w_codes = const.tile([P, 2, EMBED], U32, align_bytes=64)
+        w_scales = const.tile([P, 2, EMBED], U8, align_bytes=64)
+        for which, w in enumerate((Wq, Wk)):
+            w_raw = weights.tile([P, PACK, EMBED], BF16)
+            for u in range(2):
+                nc.scalar.dma_start(
+                    out=w_raw[:, 2 * u : 2 * u + 2, :],
+                    in_=w[256 * u : 256 * u + 256, :].rearrange("(q e) c -> q e c", e=2),
+                )
+            w_grouped = weights.tile([P, EMBED, PACK], BF16, align_bytes=64)
+            nc.vector.tensor_copy(out=w_grouped[:], in_=w_raw[:].rearrange("p t c -> p c t"))
+            nc.vector.quantize_mx(
+                out=w_codes[:, which, :].bitcast(FP8X4),
+                scales=w_scales[:, which, :],
+                in_=w_grouped[:].rearrange("p c t -> p (c t)"),
+            )
+
+        bias_rows = const.tile([P, P], BF16)
+        nc.vector.memset(bias_rows[:], 0.0)
+        nc.scalar.dma_start(out=bias_rows[0:FEATURE_TILES, :], in_=bq.rearrange("(t p) -> t p", p=P))
+        nc.scalar.dma_start(
+            out=bias_rows[FEATURE_TILES : 2 * FEATURE_TILES, :], in_=bk.rearrange("(t p) -> t p", p=P)
+        )
+        bias_bank = work.tile([P, P], BF16, tag="work")
+        nc.tensor.transpose(out=bias_bank[:], in_=bias_rows[:], identity=ident_bf[:])
+        bias_cols = const.tile([P, 2 * FEATURE_TILES], F32)
+        nc.vector.tensor_copy(out=bias_cols[:], in_=bias_bank[:, 0 : 2 * FEATURE_TILES])
+
+        mask_rows = const.tile([P, COLS], BF16)
+        nc.vector.memset(mask_rows[:], 0.0)
+        nc.scalar.dma_start(out=mask_rows[0:ROWS, :], in_=mask)
+
+        x_codes = const.tile([P, ROW_GROUPS, COL_HALVES, TOKENS], U32, align_bytes=64)
+        x_scales = const.tile([P, ROW_GROUPS, COL_HALVES, TOKENS], U8, align_bytes=64)
+        keep = const.tile([P, ROW_GROUPS, COL_HALVES, TOKENS], F32)
+        code_sets = []
+        for s in range(CODE_SETS):
+            code_set = {
+                "q_head0": const.tile([P, ROW_GROUPS, COLS], U32, name="q_head0_%d" % s, align_bytes=64),
+                "q_head1": const.tile([P, ROW_GROUPS, COLS], U32, name="q_head1_%d" % s, align_bytes=64),
+                "q_scales": const.tile([P, ROW_GROUPS, COLS], U8, name="q_scales_%d" % s, align_bytes=64),
+                "k_codes": const.tile([P, ROW_GROUPS, COLS], U32, name="k_codes_%d" % s, align_bytes=64),
+                "k_scales": const.tile([P, ROW_GROUPS, COLS], U8, name="k_scales_%d" % s, align_bytes=64),
+            }
+            nc.vector.memset(code_set["q_head1"][0:HALF].bitcast(I32), 0)
+            code_sets.append(code_set)
+
+        def prepare_x(g, half):
+            x_sb = x_pool.tile([P, PACK * EMBED], BF16)
+            nc.sync.dma_start(
+                out=x_sb[:].rearrange("p (r e) -> p r e", r=PACK),
+                in_=x[PACK * g : PACK * g + PACK, P * half : P * half + P, :].rearrange("r p e -> p r e"),
+            )
+            x_words = x_sb[:].bitcast(F32)
+            x_grouped = grouped_pool.tile([P, TOKENS * PACK], BF16, align_bytes=64)
+            grouped_words = x_grouped[:].bitcast(F32).rearrange("p (i r u) -> p i r u", r=PACK, u=2)
+            for pair in range(2):
+                x_bank = work.tile([P, 2, 2, P], F32, tag="work")
+                for r in range(2):
+                    for u in range(2):
+                        first = (2 * pair + r) * (EMBED // 2) + u * P
+                        nc.tensor.transpose(
+                            out=x_bank[:, r, u, :], in_=x_words[:, first : first + P], identity=ident_f32[:]
+                        )
+                nc.scalar.copy(
+                    out=grouped_words[:, :, 2 * pair : 2 * pair + 2, :],
+                    in_=x_bank[:].rearrange("p r u i -> p i r u"),
+                )
+            nc.vector.quantize_mx(
+                out=x_codes[:, g, half, :].bitcast(FP8X4), scales=x_scales[:, g, half, :], in_=x_grouped[:]
+            )
+            mask_bank = work.tile([P, PACK, P], F32, tag="work")
+            for r in range(PACK):
+                row = PACK * g + r
+                nc.tensor.matmul(
+                    out=mask_bank[:, r, :],
+                    lhsT=ident_bf[:, row : row + 1].to_broadcast([P, P]),
+                    rhs=mask_rows[:, P * half : P * half + P],
+                    start=True,
+                    stop=True,
+                )
+            nc.scalar.activation(
+                out=keep[:, g, half, :].rearrange("p (i r) -> p i r", r=PACK),
+                in_=mask_bank[:].rearrange("p r i -> p i r"),
+                func=ACT.Copy,
+                scale=-SCALING,
+                bias=SCALING,
+            )
+
+        def project(ft, g):
+            code_set = code_sets[ft % CODE_SETS]
+            features = slice(P * ft, P * ft + P)
+            q_bf = qk_pool.tile([P, COL_HALVES, TOKENS], BF16, align_bytes=64)
+            k_bf = qk_pool.tile([P, COL_HALVES, TOKENS], BF16, align_bytes=64)
+            for half in range(COL_HALVES):
+                q_bank = work.tile([P, TOKENS], F32, tag="work")
+                k_bank = work.tile([P, TOKENS], F32, tag="work")
+                for which, bank in enumerate((q_bank, k_bank)):
+                    nc.tensor.matmul_mx(
+                        out=bank[:],
+                        lhsT=w_codes[:, which, features].bitcast(FP8X4),
+                        lhsT_scale=w_scales[:, which, features],
+                        rhs=x_codes[:, g, half, :].bitcast(FP8X4),
+                        rhs_scale=x_scales[:, g, half, :],
+                        start=True,
+                        stop=True,
+                    )
+                nc.vector.scalar_tensor_tensor(
+                    out=q_bf[:, half, :],
+                    in0=q_bank[:],
+                    scalar=bias_cols[:, ft : ft + 1],
+                    in1=keep[:, g, half, :],
+                    op0=ADD,
+                    op1=MULT,
+                )
+                nc.scalar.activation(
+                    out=k_bf[:, half, :],
+                    in_=k_bank[:],
+                    func=ACT.Identity,
+                    bias=bias_cols[:, FEATURE_TILES + ft : FEATURE_TILES + ft + 1],
+                    scale=1.0,
+                )
+            nc.vector.quantize_mx(
+                out=code_set["q_head0"][:, g, :].bitcast(FP8X4),
+                scales=code_set["q_scales"][:, g, :],
+                in_=q_bf[:].rearrange("p h n -> p (h n)"),
+            )
+            nc.vector.quantize_mx(
+                out=code_set["k_codes"][:, g, :].bitcast(FP8X4),
+                scales=code_set["k_scales"][:, g, :],
+                in_=k_bf[:].rearrange("p h n -> p (h n)"),
+            )
+            if g % SPLIT == SPLIT - 1:
+                groups = slice(g + 1 - SPLIT, g + 1)
+                nc.vector.tensor_copy(
+                    out=code_set["q_head1"][HALF:P, groups, :].bitcast(I32),
+                    in_=code_set["q_head0"][HALF:P, groups, :].bitcast(I32),
+                )
+                nc.vector.memset(code_set["q_head0"][HALF:P, groups, :].bitcast(I32), 0)
+
+        def logits(ft, i_tile):
+            code_set = code_sets[ft % CODE_SETS]
+            queries = slice(P * i_tile, P * i_tile + P)
+            acc = logit_banks.tile([P, 2, COLS], F32)
+            for head in range(2):
+                for g in range(ROW_GROUPS):
+                    nc.tensor.matmul_mx(
+                        out=acc[:, head, :],
+                        lhsT=code_set["q_head%d" % head][:, g, queries].bitcast(FP8X4),
+                        lhsT_scale=code_set["q_scales"][:, g, queries],
+                        rhs=code_set["k_codes"][:, g, :].bitcast(FP8X4),
+                        rhs_scale=code_set["k_scales"][:, g, :],
+                        start=(g == 0),
+                        stop=(g == ROW_GROUPS - 1),
+                    )
+            result = out_pool.tile([P, 2, COLS], F32)
+            nc.scalar.copy(out=result[:], in_=acc[:])
+            nc.sync.dma_start(
+                out=out[2 * ft : 2 * ft + 2, queries, :].rearrange("h i j -> i h j"), in_=result[:]
+            )
+
+        for g in range(ROW_GROUPS):
+            for half in range(COL_HALVES):
+                prepare_x(g, half)
+            for ft in range(STREAMED_TILES):
+                project(ft, g)
+
+        step = 0
+        for ft in range(STREAMED_TILES, FEATURE_TILES):
+            for g in range(ROW_GROUPS):
+                ready = step // 2
+                if step % 2 == 0 and ready // COL_HALVES < ft:
+                    logits(ready // COL_HALVES, ready % COL_HALVES)
+                project(ft, g)
+                step += 1
+        for i_tile in range(COL_HALVES):
+            logits(FEATURE_TILES - 1, i_tile)

@@ -19,14 +19,21 @@ SCALING = HEAD_DIM**-0.5 / ROWS**0.5
 
 P = 128
 PACK = 4
+BANK = 512
 ROW_GROUPS = ROWS // PACK
 COL_HALVES = COLS // P
 FEATURE_TILES = EMBED // P
 HALF = P // 2
 TOKENS = P * PACK
-STREAMED_TILES = 2
-CODE_SETS = 3
-SPLIT = 4
+UNITS_PER_TILE = ROW_GROUPS * COL_HALVES
+UNITS = FEATURE_TILES * UNITS_PER_TILE
+CODE_SETS = 2
+BATCH = 2
+BATCHES = ROW_GROUPS // BATCH
+LOGIT_GROUPS = 2 * COL_HALVES
+X_LOADS_AHEAD = 6
+RING_WHILE_X_STREAMS = 8
+RING_BESIDE_LOGITS = 4
 
 FLOPS = 2 * ROWS * COLS * EMBED * 2 * EMBED + 2 * HEADS * COLS * COLS * ROWS * HEAD_DIM
 
@@ -36,53 +43,65 @@ def tile_rowselfattention_pa_t_kernel(tc, x, mask, Wq, bq, Wk, bk, out):
     with ExitStack() as stack:
         const = stack.enter_context(tc.tile_pool(name="const", bufs=1))
         weights = stack.enter_context(tc.tile_pool(name="weights", bufs=2))
-        x_pool = stack.enter_context(tc.tile_pool(name="x_pool", bufs=4))
+        x_pool = stack.enter_context(tc.tile_pool(name="x_pool", bufs=X_LOADS_AHEAD))
         grouped_pool = stack.enter_context(tc.tile_pool(name="grouped_pool", bufs=3))
         qk_pool = stack.enter_context(tc.tile_pool(name="qk_pool", bufs=3))
-        out_pool = stack.enter_context(tc.tile_pool(name="out_pool", bufs=2))
-        work = stack.enter_context(tc.psum_pool(name="work", bufs=6))
-        logit_banks = stack.enter_context(tc.psum_pool(name="logit_banks", bufs=2))
+        staging_pool = stack.enter_context(tc.tile_pool(name="staging_pool", bufs=4))
+        out_pool = stack.enter_context(tc.tile_pool(name="out_pool", bufs=4))
+        psum = stack.enter_context(tc.psum_pool(name="psum", bufs=1))
+        stack.enter_context(tc.manual_schedule())
 
-        ident_f32 = const.tile([P, P], F32)
-        make_identity(nc, ident_f32[:])
-        ident_bf = const.tile([P, P], BF16)
-        nc.vector.tensor_copy(out=ident_bf[:], in_=ident_f32[:])
+        banks_taken = [0]
 
-        w_codes = const.tile([P, 2, EMBED], U32, align_bytes=64)
-        w_scales = const.tile([P, 2, EMBED], U8, align_bytes=64)
-        for which, w in enumerate((Wq, Wk)):
-            w_raw = weights.tile([P, PACK, EMBED], BF16)
-            for u in range(2):
-                nc.scalar.dma_start(
-                    out=w_raw[:, 2 * u : 2 * u + 2, :],
-                    in_=w[256 * u : 256 * u + 256, :].rearrange("(q e) c -> q e c", e=2),
-                )
-            w_grouped = weights.tile([P, EMBED, PACK], BF16, align_bytes=64)
-            nc.vector.tensor_copy(out=w_grouped[:], in_=w_raw[:].rearrange("p t c -> p c t"))
-            nc.vector.quantize_mx(
-                out=w_codes[:, which, :].bitcast(FP8X4),
-                scales=w_scales[:, which, :],
-                in_=w_grouped[:].rearrange("p c t -> p (c t)"),
+        def bank(index):
+            return psum.tile([P, BANK], F32, name="bank%d" % index, tag="bank%d" % index)
+
+        def next_bank(ring):
+            index = banks_taken[0] % ring
+            banks_taken[0] += 1
+            return bank(index)
+
+        x_tiles = {}
+
+        def load_x(t):
+            g, half = t // COL_HALVES, t % COL_HALVES
+            x_sb = x_pool.tile([P, PACK * EMBED], BF16, name="x_sb")
+            nc.sync.dma_start(
+                out=x_sb[:].rearrange("p (r e) -> p r e", r=PACK),
+                in_=x[PACK * g : PACK * g + PACK, P * half : P * half + P, :].rearrange("r p e -> p r e"),
             )
+            x_tiles[t] = x_sb
 
+        for t in range(2):
+            load_x(t)
         bias_rows = const.tile([P, P], BF16)
+        mask_rows = const.tile([P, COLS], BF16)
         nc.vector.memset(bias_rows[:], 0.0)
+        nc.vector.memset(mask_rows[:], 0.0)
+        nc.scalar.dma_start(out=mask_rows[0:ROWS, :], in_=mask)
         nc.scalar.dma_start(out=bias_rows[0:FEATURE_TILES, :], in_=bq.rearrange("(t p) -> t p", p=P))
         nc.scalar.dma_start(
             out=bias_rows[FEATURE_TILES : 2 * FEATURE_TILES, :], in_=bk.rearrange("(t p) -> t p", p=P)
         )
-        bias_bank = work.tile([P, P], BF16, tag="work")
-        nc.tensor.transpose(out=bias_bank[:], in_=bias_rows[:], identity=ident_bf[:])
+        w_raw = []
+        for which, w in enumerate((Wq, Wk)):
+            raw = weights.tile([P, PACK, EMBED], BF16, name="w_raw")
+            nc.scalar.dma_start(
+                out=raw[:].rearrange("p (u e) c -> p u (e c)", u=2),
+                in_=w.rearrange("(u q e) c -> q u (e c)", u=2, e=2),
+            )
+            w_raw.append(raw)
+
+        ident_f32 = const.tile([P, P], F32)
+        make_identity(nc, ident_f32[:])
+        ident_bf = const.tile([P, P], BF16)
+
+        w_codes = const.tile([P, 2, EMBED], U32, align_bytes=64)
+        w_scales = const.tile([P, 2, EMBED], U8, align_bytes=64)
         bias_cols = const.tile([P, 2 * FEATURE_TILES], F32)
-        nc.vector.tensor_copy(out=bias_cols[:], in_=bias_bank[:, 0 : 2 * FEATURE_TILES])
-
-        mask_rows = const.tile([P, COLS], BF16)
-        nc.vector.memset(mask_rows[:], 0.0)
-        nc.scalar.dma_start(out=mask_rows[0:ROWS, :], in_=mask)
-
-        x_codes = const.tile([P, ROW_GROUPS, COL_HALVES, TOKENS], U32, align_bytes=64)
-        x_scales = const.tile([P, ROW_GROUPS, COL_HALVES, TOKENS], U8, align_bytes=64)
-        keep = const.tile([P, ROW_GROUPS, COL_HALVES, TOKENS], F32)
+        x_codes = const.tile([P, UNITS_PER_TILE, TOKENS], U32, align_bytes=64)
+        x_scales = const.tile([P, UNITS_PER_TILE, TOKENS], U8, align_bytes=64)
+        keep = const.tile([P, UNITS_PER_TILE, TOKENS], F32)
         code_sets = []
         for s in range(CODE_SETS):
             code_set = {
@@ -92,86 +111,133 @@ def tile_rowselfattention_pa_t_kernel(tc, x, mask, Wq, bq, Wk, bk, out):
                 "k_codes": const.tile([P, ROW_GROUPS, COLS], U32, name="k_codes_%d" % s, align_bytes=64),
                 "k_scales": const.tile([P, ROW_GROUPS, COLS], U8, name="k_scales_%d" % s, align_bytes=64),
             }
+            nc.vector.memset(code_set["q_head0"][HALF:P].bitcast(I32), 0)
+            if s == 0:
+                nc.vector.tensor_copy(out=ident_bf[:], in_=ident_f32[:])
             nc.vector.memset(code_set["q_head1"][0:HALF].bitcast(I32), 0)
             code_sets.append(code_set)
 
-        def prepare_x(g, half):
-            x_sb = x_pool.tile([P, PACK * EMBED], BF16)
-            nc.sync.dma_start(
-                out=x_sb[:].rearrange("p (r e) -> p r e", r=PACK),
-                in_=x[PACK * g : PACK * g + PACK, P * half : P * half + P, :].rearrange("r p e -> p r e"),
-            )
-            x_words = x_sb[:].bitcast(F32)
-            x_grouped = grouped_pool.tile([P, TOKENS * PACK], BF16, align_bytes=64)
-            grouped_words = x_grouped[:].bitcast(F32).rearrange("p (i r u) -> p i r u", r=PACK, u=2)
+        x_banks = {}
+        grouped_tiles = {}
+        proj_banks = {}
+        qk_tiles = {}
+        staging = {}
+        accs = {}
+
+        def transpose_x(t):
+            g, half = t // COL_HALVES, t % COL_HALVES
+            x_words = x_tiles[t][:].bitcast(F32)
+            pair_banks = []
             for pair in range(2):
-                x_bank = work.tile([P, 2, 2, P], F32, tag="work")
+                x_bank = next_bank(RING_WHILE_X_STREAMS)
+                x_view = x_bank[:].rearrange("p (r u i) -> p r u i", r=2, u=2)
                 for r in range(2):
                     for u in range(2):
                         first = (2 * pair + r) * (EMBED // 2) + u * P
                         nc.tensor.transpose(
-                            out=x_bank[:, r, u, :], in_=x_words[:, first : first + P], identity=ident_f32[:]
+                            out=x_view[:, r, u, :], in_=x_words[:, first : first + P], identity=ident_f32[:]
                         )
-                nc.scalar.copy(
-                    out=grouped_words[:, :, 2 * pair : 2 * pair + 2, :],
-                    in_=x_bank[:].rearrange("p r u i -> p i r u"),
-                )
-            nc.vector.quantize_mx(
-                out=x_codes[:, g, half, :].bitcast(FP8X4), scales=x_scales[:, g, half, :], in_=x_grouped[:]
-            )
-            mask_bank = work.tile([P, PACK, P], F32, tag="work")
+                pair_banks.append(x_view)
+            mask_bank = next_bank(RING_WHILE_X_STREAMS)
+            mask_view = mask_bank[:].rearrange("p (r i) -> p r i", r=PACK)
             for r in range(PACK):
                 row = PACK * g + r
                 nc.tensor.matmul(
-                    out=mask_bank[:, r, :],
+                    out=mask_view[:, r, :],
                     lhsT=ident_bf[:, row : row + 1].to_broadcast([P, P]),
                     rhs=mask_rows[:, P * half : P * half + P],
                     start=True,
                     stop=True,
                 )
-            nc.scalar.activation(
-                out=keep[:, g, half, :].rearrange("p (i r) -> p i r", r=PACK),
-                in_=mask_bank[:].rearrange("p r i -> p i r"),
-                func=ACT.Copy,
-                scale=-SCALING,
-                bias=SCALING,
+            x_banks[t] = (pair_banks, mask_view)
+
+        def evacuate_x(t):
+            pair_banks, mask_view = x_banks[t]
+            x_grouped = grouped_pool.tile([P, TOKENS * PACK], BF16, name="x_grouped", align_bytes=64)
+            grouped_words = x_grouped[:].bitcast(F32).rearrange("p (i r u) -> p i r u", r=PACK, u=2)
+            for pair in range(2):
+                nc.scalar.copy(
+                    out=grouped_words[:, :, 2 * pair : 2 * pair + 2, :],
+                    in_=pair_banks[pair].rearrange("p r u i -> p i r u"),
+                )
+            keep_view = keep[:, t, :].rearrange("p (i r) -> p i r", r=PACK)
+            if t % COL_HALVES == 0:
+                nc.scalar.activation(
+                    out=keep_view,
+                    in_=mask_view.rearrange("p r i -> p i r"),
+                    func=ACT.Copy,
+                    scale=-SCALING,
+                    bias=SCALING,
+                )
+            else:
+                nc.vector.tensor_scalar(
+                    out=keep_view,
+                    in0=mask_view.rearrange("p r i -> p i r"),
+                    scalar1=-SCALING,
+                    scalar2=SCALING,
+                    op0=MULT,
+                    op1=ADD,
+                )
+            grouped_tiles[t] = x_grouped
+
+        def quantise_x(t):
+            nc.vector.quantize_mx(
+                out=x_codes[:, t, :].bitcast(FP8X4), scales=x_scales[:, t, :], in_=grouped_tiles[t][:]
             )
 
-        def project(ft, g):
-            code_set = code_sets[ft % CODE_SETS]
+        def project(u):
+            ft, t = u // UNITS_PER_TILE, u % UNITS_PER_TILE
             features = slice(P * ft, P * ft + P)
-            q_bf = qk_pool.tile([P, COL_HALVES, TOKENS], BF16, align_bytes=64)
-            k_bf = qk_pool.tile([P, COL_HALVES, TOKENS], BF16, align_bytes=64)
-            for half in range(COL_HALVES):
-                q_bank = work.tile([P, TOKENS], F32, tag="work")
-                k_bank = work.tile([P, TOKENS], F32, tag="work")
-                for which, bank in enumerate((q_bank, k_bank)):
-                    nc.tensor.matmul_mx(
-                        out=bank[:],
-                        lhsT=w_codes[:, which, features].bitcast(FP8X4),
-                        lhsT_scale=w_scales[:, which, features],
-                        rhs=x_codes[:, g, half, :].bitcast(FP8X4),
-                        rhs_scale=x_scales[:, g, half, :],
-                        start=True,
-                        stop=True,
-                    )
-                nc.vector.scalar_tensor_tensor(
-                    out=q_bf[:, half, :],
-                    in0=q_bank[:],
-                    scalar=bias_cols[:, ft : ft + 1],
-                    in1=keep[:, g, half, :],
-                    op0=ADD,
-                    op1=MULT,
+            ring = RING_WHILE_X_STREAMS if ft == 0 else RING_BESIDE_LOGITS
+            pair = []
+            for which in range(2):
+                acc = next_bank(ring)
+                nc.tensor.matmul_mx(
+                    out=acc[:],
+                    lhsT=w_codes[:, which, features].bitcast(FP8X4),
+                    lhsT_scale=w_scales[:, which, features],
+                    rhs=x_codes[:, t, :].bitcast(FP8X4),
+                    rhs_scale=x_scales[:, t, :],
+                    start=True,
+                    stop=True,
                 )
-                nc.scalar.activation(
-                    out=k_bf[:, half, :],
-                    in_=k_bank[:],
-                    func=ACT.Identity,
-                    bias=bias_cols[:, FEATURE_TILES + ft : FEATURE_TILES + ft + 1],
-                    scale=1.0,
+                pair.append(acc)
+            proj_banks[u] = pair
+
+        def finish(u):
+            ft, t = u // UNITS_PER_TILE, u % UNITS_PER_TILE
+            half = t % COL_HALVES
+            if half == 0:
+                qk_tiles[u // COL_HALVES] = (
+                    qk_pool.tile([P, COL_HALVES, TOKENS], BF16, name="q_bf", align_bytes=64),
+                    qk_pool.tile([P, COL_HALVES, TOKENS], BF16, name="k_bf", align_bytes=64),
                 )
+            q_bf, k_bf = qk_tiles[u // COL_HALVES]
+            q_bank, k_bank = proj_banks[u]
+            nc.vector.scalar_tensor_tensor(
+                out=q_bf[:, half, :],
+                in0=q_bank[:],
+                scalar=bias_cols[:, ft : ft + 1],
+                in1=keep[:, t, :],
+                op0=ADD,
+                op1=MULT,
+            )
+            nc.scalar.activation(
+                out=k_bf[:, half, :],
+                in_=k_bank[:],
+                func=ACT.Identity,
+                bias=bias_cols[:, FEATURE_TILES + ft : FEATURE_TILES + ft + 1],
+                scale=1.0,
+            )
+
+        def quantise_qk(ft, g):
+            code_set = code_sets[ft % CODE_SETS]
+            q_bf, k_bf = qk_tiles[ft * ROW_GROUPS + g]
+            if g % BATCH == 0:
+                staging[ft] = staging_pool.tile([P, BATCH, COLS], U32, name="q_codes", align_bytes=64)
+            q_codes = staging[ft]
             nc.vector.quantize_mx(
-                out=code_set["q_head0"][:, g, :].bitcast(FP8X4),
+                out=q_codes[:, g % BATCH, :].bitcast(FP8X4),
                 scales=code_set["q_scales"][:, g, :],
                 in_=q_bf[:].rearrange("p h n -> p (h n)"),
             )
@@ -180,48 +246,84 @@ def tile_rowselfattention_pa_t_kernel(tc, x, mask, Wq, bq, Wk, bk, out):
                 scales=code_set["k_scales"][:, g, :],
                 in_=k_bf[:].rearrange("p h n -> p (h n)"),
             )
-            if g % SPLIT == SPLIT - 1:
-                groups = slice(g + 1 - SPLIT, g + 1)
-                nc.vector.tensor_copy(
-                    out=code_set["q_head1"][HALF:P, groups, :].bitcast(I32),
-                    in_=code_set["q_head0"][HALF:P, groups, :].bitcast(I32),
+            if g % BATCH == BATCH - 1:
+                groups = slice(g + 1 - BATCH, g + 1)
+                nc.sync.dma_start(
+                    out=code_set["q_head0"][0:HALF, groups, :].bitcast(I32), in_=q_codes[0:HALF].bitcast(I32)
                 )
-                nc.vector.memset(code_set["q_head0"][HALF:P, groups, :].bitcast(I32), 0)
+                nc.sync.dma_start(
+                    out=code_set["q_head1"][HALF:P, groups, :].bitcast(I32), in_=q_codes[HALF:P].bitcast(I32)
+                )
 
-        def logits(ft, i_tile):
+        def logits_piece(ft, v):
             code_set = code_sets[ft % CODE_SETS]
+            batch, n = v // LOGIT_GROUPS, v % LOGIT_GROUPS
+            i_tile, head = n // 2, n % 2
             queries = slice(P * i_tile, P * i_tile + P)
-            acc = logit_banks.tile([P, 2, COLS], F32)
-            for head in range(2):
-                for g in range(ROW_GROUPS):
-                    nc.tensor.matmul_mx(
-                        out=acc[:, head, :],
-                        lhsT=code_set["q_head%d" % head][:, g, queries].bitcast(FP8X4),
-                        lhsT_scale=code_set["q_scales"][:, g, queries],
-                        rhs=code_set["k_codes"][:, g, :].bitcast(FP8X4),
-                        rhs_scale=code_set["k_scales"][:, g, :],
-                        start=(g == 0),
-                        stop=(g == ROW_GROUPS - 1),
-                    )
-            result = out_pool.tile([P, 2, COLS], F32)
-            nc.scalar.copy(out=result[:], in_=acc[:])
-            nc.sync.dma_start(
-                out=out[2 * ft : 2 * ft + 2, queries, :].rearrange("h i j -> i h j"), in_=result[:]
+            if batch == 0:
+                accs[n] = bank(RING_BESIDE_LOGITS + n)
+            for g in range(BATCH * batch, BATCH * batch + BATCH):
+                nc.tensor.matmul_mx(
+                    out=accs[n][:, 0:COLS],
+                    lhsT=code_set["q_head%d" % head][:, g, queries].bitcast(FP8X4),
+                    lhsT_scale=code_set["q_scales"][:, g, queries],
+                    rhs=code_set["k_codes"][:, g, :].bitcast(FP8X4),
+                    rhs_scale=code_set["k_scales"][:, g, :],
+                    start=(g == 0),
+                    stop=(g == ROW_GROUPS - 1),
+                )
+
+        def store_logits(ft, n):
+            i_tile, head = n // 2, n % 2
+            result = out_pool.tile([P, COLS], F32, name="result")
+            nc.scalar.copy(out=result[:], in_=accs[n][:, 0:COLS])
+            nc.sync.dma_start(out=out[2 * ft + head, P * i_tile : P * i_tile + P, :], in_=result[:])
+
+        for t in range(2, X_LOADS_AHEAD):
+            load_x(t)
+        transpose_x(0)
+        bias_bank = psum.tile([P, P], BF16, name="bias_bank", tag="bank7")
+        nc.tensor.transpose(out=bias_bank[:], in_=bias_rows[:], identity=ident_bf[:])
+        transpose_x(1)
+        w_grouped = []
+        for which in range(2):
+            grouped = weights.tile([P, EMBED, PACK], BF16, name="w_grouped", align_bytes=64)
+            nc.vector.tensor_copy(out=grouped[:], in_=w_raw[which][:].rearrange("p t c -> p c t"))
+            w_grouped.append(grouped)
+        for which in range(2):
+            nc.vector.quantize_mx(
+                out=w_codes[:, which, :].bitcast(FP8X4),
+                scales=w_scales[:, which, :],
+                in_=w_grouped[which][:].rearrange("p c t -> p (c t)"),
             )
+        nc.vector.tensor_copy(out=bias_cols[:], in_=bias_bank[:, 0 : 2 * FEATURE_TILES])
+        for t in range(2):
+            evacuate_x(t)
+            quantise_x(t)
+        project(0)
 
-        for g in range(ROW_GROUPS):
-            for half in range(COL_HALVES):
-                prepare_x(g, half)
-            for ft in range(STREAMED_TILES):
-                project(ft, g)
+        for u in range(UNITS):
+            ft, v = u // UNITS_PER_TILE, u % UNITS_PER_TILE
+            if u + X_LOADS_AHEAD < UNITS_PER_TILE:
+                load_x(u + X_LOADS_AHEAD)
+            if u + 2 < UNITS_PER_TILE:
+                transpose_x(u + 2)
+            if u + 1 < UNITS:
+                project(u + 1)
+            if ft > 0:
+                logits_piece(ft - 1, v)
+            finish(u)
+            if u >= COL_HALVES and u % COL_HALVES == 0:
+                done = u // COL_HALVES - 1
+                quantise_qk(done // ROW_GROUPS, done % ROW_GROUPS)
+            if u + 2 < UNITS_PER_TILE:
+                evacuate_x(u + 2)
+                quantise_x(u + 2)
+            if ft > 0 and v // LOGIT_GROUPS == BATCHES - 1:
+                store_logits(ft - 1, v % LOGIT_GROUPS)
 
-        step = 0
-        for ft in range(STREAMED_TILES, FEATURE_TILES):
-            for g in range(ROW_GROUPS):
-                ready = step // 2
-                if step % 2 == 0 and ready // COL_HALVES < ft:
-                    logits(ready // COL_HALVES, ready % COL_HALVES)
-                project(ft, g)
-                step += 1
-        for i_tile in range(COL_HALVES):
-            logits(FEATURE_TILES - 1, i_tile)
+        quantise_qk(FEATURE_TILES - 1, ROW_GROUPS - 1)
+        for v in range(UNITS_PER_TILE):
+            logits_piece(FEATURE_TILES - 1, v)
+            if v // LOGIT_GROUPS == BATCHES - 1:
+                store_logits(FEATURE_TILES - 1, v % LOGIT_GROUPS)

@@ -46,7 +46,6 @@ def tile_rowselfattention_pa_t_kernel(tc, x, mask, Wq, bq, Wk, bk, out):
         x_pool = stack.enter_context(tc.tile_pool(name="x_pool", bufs=X_LOADS_AHEAD))
         grouped_pool = stack.enter_context(tc.tile_pool(name="grouped_pool", bufs=3))
         qk_pool = stack.enter_context(tc.tile_pool(name="qk_pool", bufs=3))
-        staging_pool = stack.enter_context(tc.tile_pool(name="staging_pool", bufs=4))
         out_pool = stack.enter_context(tc.tile_pool(name="out_pool", bufs=4))
         psum = stack.enter_context(tc.psum_pool(name="psum", bufs=1))
         stack.enter_context(tc.manual_schedule())
@@ -105,23 +104,24 @@ def tile_rowselfattention_pa_t_kernel(tc, x, mask, Wq, bq, Wk, bk, out):
         code_sets = []
         for s in range(CODE_SETS):
             code_set = {
-                "q_head0": const.tile([P, ROW_GROUPS, COLS], U32, name="q_head0_%d" % s, align_bytes=64),
-                "q_head1": const.tile([P, ROW_GROUPS, COLS], U32, name="q_head1_%d" % s, align_bytes=64),
+                "q_codes": const.tile([P, ROW_GROUPS, COLS], U32, name="q_codes_%d" % s, align_bytes=64),
                 "q_scales": const.tile([P, ROW_GROUPS, COLS], U8, name="q_scales_%d" % s, align_bytes=64),
+                "q_scales_head0": const.tile([P, ROW_GROUPS, COLS], U8, name="q_scales_head0_%d" % s, align_bytes=64),
+                "q_scales_head1": const.tile([P, ROW_GROUPS, COLS], U8, name="q_scales_head1_%d" % s, align_bytes=64),
                 "k_codes": const.tile([P, ROW_GROUPS, COLS], U32, name="k_codes_%d" % s, align_bytes=64),
                 "k_scales": const.tile([P, ROW_GROUPS, COLS], U8, name="k_scales_%d" % s, align_bytes=64),
             }
-            nc.vector.memset(code_set["q_head0"][HALF:P].bitcast(I32), 0)
+            nc.gpsimd.memset(code_set["q_scales"][:].bitcast(I32), 0)
+            nc.gpsimd.memset(code_set["q_scales_head0"][HALF:P].bitcast(I32), 0)
+            nc.gpsimd.memset(code_set["q_scales_head1"][0:HALF].bitcast(I32), 0)
             if s == 0:
                 nc.vector.tensor_copy(out=ident_bf[:], in_=ident_f32[:])
-            nc.vector.memset(code_set["q_head1"][0:HALF].bitcast(I32), 0)
             code_sets.append(code_set)
 
         x_banks = {}
         grouped_tiles = {}
         proj_banks = {}
         qk_tiles = {}
-        staging = {}
         accs = {}
 
         def transpose_x(t):
@@ -233,11 +233,8 @@ def tile_rowselfattention_pa_t_kernel(tc, x, mask, Wq, bq, Wk, bk, out):
         def quantise_qk(ft, g):
             code_set = code_sets[ft % CODE_SETS]
             q_bf, k_bf = qk_tiles[ft * ROW_GROUPS + g]
-            if g % BATCH == 0:
-                staging[ft] = staging_pool.tile([P, BATCH, COLS], U32, name="q_codes", align_bytes=64)
-            q_codes = staging[ft]
             nc.vector.quantize_mx(
-                out=q_codes[:, g % BATCH, :].bitcast(FP8X4),
+                out=code_set["q_codes"][:, g, :].bitcast(FP8X4),
                 scales=code_set["q_scales"][:, g, :],
                 in_=q_bf[:].rearrange("p h n -> p (h n)"),
             )
@@ -249,10 +246,12 @@ def tile_rowselfattention_pa_t_kernel(tc, x, mask, Wq, bq, Wk, bk, out):
             if g % BATCH == BATCH - 1:
                 groups = slice(g + 1 - BATCH, g + 1)
                 nc.sync.dma_start(
-                    out=code_set["q_head0"][0:HALF, groups, :].bitcast(I32), in_=q_codes[0:HALF].bitcast(I32)
+                    out=code_set["q_scales_head0"][0:HALF, groups, :].bitcast(I32),
+                    in_=code_set["q_scales"][0:HALF, groups, :].bitcast(I32),
                 )
                 nc.sync.dma_start(
-                    out=code_set["q_head1"][HALF:P, groups, :].bitcast(I32), in_=q_codes[HALF:P].bitcast(I32)
+                    out=code_set["q_scales_head1"][HALF:P, groups, :].bitcast(I32),
+                    in_=code_set["q_scales"][HALF:P, groups, :].bitcast(I32),
                 )
 
         def logits_piece(ft, v):
@@ -265,8 +264,8 @@ def tile_rowselfattention_pa_t_kernel(tc, x, mask, Wq, bq, Wk, bk, out):
             for g in range(BATCH * batch, BATCH * batch + BATCH):
                 nc.tensor.matmul_mx(
                     out=accs[n][:, 0:COLS],
-                    lhsT=code_set["q_head%d" % head][:, g, queries].bitcast(FP8X4),
-                    lhsT_scale=code_set["q_scales"][:, g, queries],
+                    lhsT=code_set["q_codes"][:, g, queries].bitcast(FP8X4),
+                    lhsT_scale=code_set["q_scales_head%d" % head][:, g, queries],
                     rhs=code_set["k_codes"][:, g, :].bitcast(FP8X4),
                     rhs_scale=code_set["k_scales"][:, g, :],
                     start=(g == 0),

@@ -21,19 +21,23 @@ P = 128
 PACK = 4
 BANK = 512
 ROW_GROUPS = ROWS // PACK
+PAIRS = ROW_GROUPS // 2
 COL_HALVES = COLS // P
 FEATURE_TILES = EMBED // P
 HALF = P // 2
 TOKENS = P * PACK
-UNITS_PER_TILE = ROW_GROUPS * COL_HALVES
-UNITS = FEATURE_TILES * UNITS_PER_TILE
-CODE_SETS = 2
-BATCH = 2
-BATCHES = ROW_GROUPS // BATCH
-LOGIT_GROUPS = 2 * COL_HALVES
+X_UNITS = ROW_GROUPS * COL_HALVES
+UNSORTED_GROUPS = 4
+FIRST_TILES = 1
+STAGES = 3
+SPLIT_GROUPS = (3,)
+HEAD_MASKS = 4
+SETS = 2
+CODE_WORDS = 2 * COLS
+SET_WORDS = CODE_WORDS + CODE_WORDS // PACK
 X_LOADS_AHEAD = 6
-RING_WHILE_X_STREAMS = 8
-RING_BESIDE_LOGITS = 4
+PREP_AHEAD = 2
+SORT_LAG = 8
 
 FLOPS = 2 * ROWS * COLS * EMBED * 2 * EMBED + 2 * HEADS * COLS * COLS * ROWS * HEAD_DIM
 
@@ -46,7 +50,8 @@ def tile_rowselfattention_pa_t_kernel(tc, x, mask, Wq, bq, Wk, bk, out):
         x_pool = stack.enter_context(tc.tile_pool(name="x_pool", bufs=X_LOADS_AHEAD))
         grouped_pool = stack.enter_context(tc.tile_pool(name="grouped_pool", bufs=3))
         qk_pool = stack.enter_context(tc.tile_pool(name="qk_pool", bufs=3))
-        out_pool = stack.enter_context(tc.tile_pool(name="out_pool", bufs=4))
+        raw_pool = stack.enter_context(tc.tile_pool(name="raw_pool", bufs=2))
+        out_pool = stack.enter_context(tc.tile_pool(name="out_pool", bufs=2))
         psum = stack.enter_context(tc.psum_pool(name="psum", bufs=1))
         stack.enter_context(tc.manual_schedule())
 
@@ -60,6 +65,11 @@ def tile_rowselfattention_pa_t_kernel(tc, x, mask, Wq, bq, Wk, bk, out):
             banks_taken[0] += 1
             return bank(index)
 
+        def ring_of(ft, t):
+            if ft < FIRST_TILES:
+                return 8
+            return 6 if ft < FEATURE_TILES - 1 or t < 9 else 4
+
         x_tiles = {}
 
         def load_x(t):
@@ -71,57 +81,77 @@ def tile_rowselfattention_pa_t_kernel(tc, x, mask, Wq, bq, Wk, bk, out):
             )
             x_tiles[t] = x_sb
 
-        for t in range(2):
-            load_x(t)
         bias_rows = const.tile([P, P], BF16)
         mask_rows = const.tile([P, COLS], BF16)
         nc.vector.memset(bias_rows[:], 0.0)
-        nc.vector.memset(mask_rows[:], 0.0)
-        nc.scalar.dma_start(out=mask_rows[0:ROWS, :], in_=mask)
-        nc.scalar.dma_start(out=bias_rows[0:FEATURE_TILES, :], in_=bq.rearrange("(t p) -> t p", p=P))
-        nc.scalar.dma_start(
+        nc.vector.memset(mask_rows[ROWS : 2 * ROWS, :], 0.0)
+        nc.vector.memset(mask_rows[HALF:P, :], 0.0)
+        nc.sync.dma_start(out=mask_rows[0:ROWS, :], in_=mask)
+        load_x(0)
+        nc.sync.dma_start(out=bias_rows[0:FEATURE_TILES, :], in_=bq.rearrange("(t p) -> t p", p=P))
+        nc.sync.dma_start(
             out=bias_rows[FEATURE_TILES : 2 * FEATURE_TILES, :], in_=bk.rearrange("(t p) -> t p", p=P)
         )
         w_raw = []
         for which, w in enumerate((Wq, Wk)):
             raw = weights.tile([P, PACK, EMBED], BF16, name="w_raw")
-            nc.scalar.dma_start(
+            nc.sync.dma_start(
                 out=raw[:].rearrange("p (u e) c -> p u (e c)", u=2),
                 in_=w.rearrange("(u q e) c -> q u (e c)", u=2, e=2),
             )
             w_raw.append(raw)
+        for t in range(1, X_LOADS_AHEAD):
+            load_x(t)
 
         ident_f32 = const.tile([P, P], F32)
         make_identity(nc, ident_f32[:])
         ident_bf = const.tile([P, P], BF16)
+        nc.vector.tensor_copy(out=ident_bf[:], in_=ident_f32[:])
 
-        w_codes = const.tile([P, 2, EMBED], U32, align_bytes=64)
-        w_scales = const.tile([P, 2, EMBED], U8, align_bytes=64)
+        w_codes = const.tile([P, FEATURE_TILES, 2, P], U32, align_bytes=64)
+        w_scales = const.tile([P, FEATURE_TILES, 2, P], U8, align_bytes=64)
         bias_cols = const.tile([P, 2 * FEATURE_TILES], F32)
-        x_codes = const.tile([P, UNITS_PER_TILE, TOKENS], U32, align_bytes=64)
-        x_scales = const.tile([P, UNITS_PER_TILE, TOKENS], U8, align_bytes=64)
-        keep = const.tile([P, UNITS_PER_TILE, TOKENS], F32)
-        code_sets = []
-        for s in range(CODE_SETS):
-            code_set = {
-                "q_codes": const.tile([P, ROW_GROUPS, COLS], U32, name="q_codes_%d" % s, align_bytes=64),
-                "q_scales": const.tile([P, ROW_GROUPS, COLS], U8, name="q_scales_%d" % s, align_bytes=64),
-                "q_scales_head0": const.tile([P, ROW_GROUPS, COLS], U8, name="q_scales_head0_%d" % s, align_bytes=64),
-                "q_scales_head1": const.tile([P, ROW_GROUPS, COLS], U8, name="q_scales_head1_%d" % s, align_bytes=64),
-                "k_codes": const.tile([P, ROW_GROUPS, COLS], U32, name="k_codes_%d" % s, align_bytes=64),
-                "k_scales": const.tile([P, ROW_GROUPS, COLS], U8, name="k_scales_%d" % s, align_bytes=64),
-            }
-            nc.gpsimd.memset(code_set["q_scales"][:].bitcast(I32), 0)
-            nc.gpsimd.memset(code_set["q_scales_head0"][HALF:P].bitcast(I32), 0)
-            nc.gpsimd.memset(code_set["q_scales_head1"][0:HALF].bitcast(I32), 0)
-            if s == 0:
-                nc.vector.tensor_copy(out=ident_bf[:], in_=ident_f32[:])
-            code_sets.append(code_set)
+        bias_q_scaled = const.tile([P, FEATURE_TILES], F32)
+        keep_ones = const.tile([P, 1, COL_HALVES * TOKENS], BF16)
+        x_codes = const.tile([P, X_UNITS, TOKENS], U32, align_bytes=64)
+        x_scales = const.tile([P, X_UNITS, TOKENS], U8, align_bytes=64)
+        keep = const.tile([P, X_UNITS, TOKENS], F32)
+        stages = []
+        for s in range(STAGES):
+            stage = const.tile([P, SET_WORDS], U32, name="stage_%d" % s, align_bytes=64)
+            nc.gpsimd.memset(stage[:, CODE_WORDS:SET_WORDS].bitcast(I32), 0)
+            stages.append(stage)
+        sorted_sets = []
+        for s in range(SETS):
+            pairs = []
+            for pair in range(PAIRS):
+                tiles = [
+                    const.tile([P, SET_WORDS], U32, name="sorted_%d_%d_%d" % (s, pair, head), align_bytes=64)
+                    for head in range(2)
+                ]
+                nc.gpsimd.memset(tiles[0][:, CODE_WORDS:SET_WORDS].bitcast(I32), 0)
+                pairs.append(tiles)
+            sorted_sets.append(pairs)
+
+        last_codes = []
+        last_split = []
+        for m in range(UNSORTED_GROUPS):
+            codes = const.tile([P, SET_WORDS], U32, name="last_codes_%d" % m, align_bytes=64)
+            nc.gpsimd.memset(codes[:, CODE_WORDS:SET_WORDS].bitcast(I32), 0)
+            last_codes.append(codes)
+            planes = [const.tile([P, COLS], U8, name="last_split_%d_%d" % (m, head), align_bytes=64) for head in range(2)]
+            nc.gpsimd.memset(planes[0][HALF:P, :].bitcast(I32), 0)
+            nc.gpsimd.memset(planes[1][0:HALF, :].bitcast(I32), 0)
+            last_split.append(planes)
 
         x_banks = {}
         grouped_tiles = {}
         proj_banks = {}
+        q_raw_tiles = {}
+        grouped_weights = {}
+        mask_views = {}
         qk_tiles = {}
+        stages_taken = {}
         accs = {}
 
         def transpose_x(t):
@@ -129,7 +159,7 @@ def tile_rowselfattention_pa_t_kernel(tc, x, mask, Wq, bq, Wk, bk, out):
             x_words = x_tiles[t][:].bitcast(F32)
             pair_banks = []
             for pair in range(2):
-                x_bank = next_bank(RING_WHILE_X_STREAMS)
+                x_bank = next_bank(8)
                 x_view = x_bank[:].rearrange("p (r u i) -> p r u i", r=2, u=2)
                 for r in range(2):
                     for u in range(2):
@@ -138,7 +168,11 @@ def tile_rowselfattention_pa_t_kernel(tc, x, mask, Wq, bq, Wk, bk, out):
                             out=x_view[:, r, u, :], in_=x_words[:, first : first + P], identity=ident_f32[:]
                         )
                 pair_banks.append(x_view)
-            mask_bank = next_bank(RING_WHILE_X_STREAMS)
+            x_banks[t] = pair_banks
+
+        def spread_mask(t):
+            g, half = t // COL_HALVES, t % COL_HALVES
+            mask_bank = next_bank(8)
             mask_view = mask_bank[:].rearrange("p (r i) -> p r i", r=PACK)
             for r in range(PACK):
                 row = PACK * g + r
@@ -149,19 +183,22 @@ def tile_rowselfattention_pa_t_kernel(tc, x, mask, Wq, bq, Wk, bk, out):
                     start=True,
                     stop=True,
                 )
-            x_banks[t] = (pair_banks, mask_view)
+            mask_views[t] = mask_view
 
-        def evacuate_x(t):
-            pair_banks, mask_view = x_banks[t]
-            x_grouped = grouped_pool.tile([P, TOKENS * PACK], BF16, name="x_grouped", align_bytes=64)
-            grouped_words = x_grouped[:].bitcast(F32).rearrange("p (i r u) -> p i r u", r=PACK, u=2)
-            for pair in range(2):
-                nc.scalar.copy(
-                    out=grouped_words[:, :, 2 * pair : 2 * pair + 2, :],
-                    in_=pair_banks[pair].rearrange("p r u i -> p i r u"),
-                )
+        def evacuate_x(t, pair):
+            pair_banks = x_banks[t]
+            if pair == 0:
+                grouped_tiles[t] = grouped_pool.tile([P, TOKENS * PACK], BF16, name="x_grouped", align_bytes=64)
+            grouped_words = grouped_tiles[t][:].bitcast(F32).rearrange("p (i r u) -> p i r u", r=PACK, u=2)
+            nc.scalar.copy(
+                out=grouped_words[:, :, 2 * pair : 2 * pair + 2, :],
+                in_=pair_banks[pair].rearrange("p r u i -> p i r u"),
+            )
+
+        def copy_mask(t, on_scalar):
+            mask_view = mask_views[t]
             keep_view = keep[:, t, :].rearrange("p (i r) -> p i r", r=PACK)
-            if t % COL_HALVES == 0:
+            if on_scalar:
                 nc.scalar.activation(
                     out=keep_view,
                     in_=mask_view.rearrange("p r i -> p i r"),
@@ -178,151 +215,275 @@ def tile_rowselfattention_pa_t_kernel(tc, x, mask, Wq, bq, Wk, bk, out):
                     op0=MULT,
                     op1=ADD,
                 )
-            grouped_tiles[t] = x_grouped
 
         def quantise_x(t):
             nc.vector.quantize_mx(
                 out=x_codes[:, t, :].bitcast(FP8X4), scales=x_scales[:, t, :], in_=grouped_tiles[t][:]
             )
 
-        def project(u):
-            ft, t = u // UNITS_PER_TILE, u % UNITS_PER_TILE
-            features = slice(P * ft, P * ft + P)
-            ring = RING_WHILE_X_STREAMS if ft == 0 else RING_BESIDE_LOGITS
+        def interleave_weights(tile, which, copy):
+            if which == 0:
+                grouped_weights[tile] = const.tile([P, 2, P, PACK], BF16, name="w_grouped_%d" % (tile % 2), align_bytes=64)
+            columns = slice(P * tile, P * tile + P)
+            copy(
+                out=grouped_weights[tile][:, which], in_=w_raw[which][:, :, columns].rearrange("p t c -> p c t")
+            )
+
+        def quantise_weights(tile):
+            nc.vector.quantize_mx(
+                out=w_codes[:, tile].rearrange("p w c -> p (w c)").bitcast(FP8X4),
+                scales=w_scales[:, tile].rearrange("p w c -> p (w c)"),
+                in_=grouped_weights[tile][:].rearrange("p w c t -> p (w c t)"),
+            )
+
+        def prepare_weights(tile):
+            for which in range(2):
+                interleave_weights(tile, which, nc.vector.tensor_copy)
+            quantise_weights(tile)
+
+        def project(ft, t):
+            ring = ring_of(ft, t)
             pair = []
             for which in range(2):
                 acc = next_bank(ring)
                 nc.tensor.matmul_mx(
                     out=acc[:],
-                    lhsT=w_codes[:, which, features].bitcast(FP8X4),
-                    lhsT_scale=w_scales[:, which, features],
+                    lhsT=w_codes[:, ft, which, :].bitcast(FP8X4),
+                    lhsT_scale=w_scales[:, ft, which, :],
                     rhs=x_codes[:, t, :].bitcast(FP8X4),
                     rhs_scale=x_scales[:, t, :],
                     start=True,
                     stop=True,
                 )
                 pair.append(acc)
-            proj_banks[u] = pair
+            proj_banks[ft, t] = pair
 
-        def finish(u):
-            ft, t = u // UNITS_PER_TILE, u % UNITS_PER_TILE
-            half = t % COL_HALVES
+        def finish(ft, t):
+            g, half = t // COL_HALVES, t % COL_HALVES
             if half == 0:
-                qk_tiles[u // COL_HALVES] = (
-                    qk_pool.tile([P, COL_HALVES, TOKENS], BF16, name="q_bf", align_bytes=64),
-                    qk_pool.tile([P, COL_HALVES, TOKENS], BF16, name="k_bf", align_bytes=64),
+                qk_tiles[ft, g] = qk_pool.tile([P, 2, COL_HALVES, TOKENS], BF16, name="qk_bf_%d" % (ft % FIRST_TILES), align_bytes=64)
+            qk_bf = qk_tiles[ft, g]
+            q_bank, k_bank = proj_banks[ft, t]
+            if ft > 0 and g in SPLIT_GROUPS:
+                if half == 0:
+                    q_raw_tiles[ft, g] = raw_pool.tile([P, COL_HALVES, TOKENS], BF16, name="q_raw", align_bytes=64)
+                nc.scalar.activation(
+                    out=q_raw_tiles[ft, g][:, half, :],
+                    in_=q_bank[:],
+                    func=ACT.Identity,
+                    bias=bias_q_scaled[:, ft : ft + 1],
+                    scale=SCALING,
                 )
-            q_bf, k_bf = qk_tiles[u // COL_HALVES]
-            q_bank, k_bank = proj_banks[u]
-            nc.vector.scalar_tensor_tensor(
-                out=q_bf[:, half, :],
-                in0=q_bank[:],
-                scalar=bias_cols[:, ft : ft + 1],
-                in1=keep[:, t, :],
-                op0=ADD,
-                op1=MULT,
-            )
+            else:
+                nc.vector.scalar_tensor_tensor(
+                    out=qk_bf[:, 0, half, :],
+                    in0=q_bank[:],
+                    scalar=bias_cols[:, ft : ft + 1],
+                    in1=keep[:, t, :],
+                    op0=ADD,
+                    op1=MULT,
+                )
             nc.scalar.activation(
-                out=k_bf[:, half, :],
+                out=qk_bf[:, 1, half, :],
                 in_=k_bank[:],
                 func=ACT.Identity,
                 bias=bias_cols[:, FEATURE_TILES + ft : FEATURE_TILES + ft + 1],
                 scale=1.0,
             )
 
+        def make_keep_ones(index):
+            g = SPLIT_GROUPS[index]
+            nc.scalar.activation(
+                out=keep_ones[:, index, :],
+                in_=keep[:, COL_HALVES * g : COL_HALVES * g + COL_HALVES, :].rearrange("p h n -> p (h n)"),
+                func=ACT.Copy,
+                scale=1.0 / SCALING,
+            )
+
+        def mask_q(ft, g):
+            nc.vector.tensor_tensor(
+                out=qk_tiles[ft, g][:, 0].rearrange("p h n -> p (h n)"),
+                in0=q_raw_tiles[ft, g][:].rearrange("p h n -> p (h n)"),
+                in1=keep_ones[:, SPLIT_GROUPS.index(g), :],
+                op=MULT,
+            )
+
         def quantise_qk(ft, g):
-            code_set = code_sets[ft % CODE_SETS]
-            q_bf, k_bf = qk_tiles[ft * ROW_GROUPS + g]
+            pair, member = g // 2, g % 2
+            first, second = sorted_sets[ft % SETS][pair]
+            if member == 1 and not (ft == FEATURE_TILES - 1 and g >= ROW_GROUPS - UNSORTED_GROUPS):
+                stages_taken[ft, pair] = stages[len(stages_taken) % STAGES]
+            target = first if member == 0 else stages_taken.get((ft, pair))
+            place = g - (ROW_GROUPS - UNSORTED_GROUPS)
+            unsorted = ft == FEATURE_TILES - 1 and place >= 0
+            if unsorted:
+                target = last_codes[place]
             nc.vector.quantize_mx(
-                out=code_set["q_codes"][:, g, :].bitcast(FP8X4),
-                scales=code_set["q_scales"][:, g, :],
-                in_=q_bf[:].rearrange("p h n -> p (h n)"),
+                out=target[:, 0:CODE_WORDS].bitcast(FP8X4),
+                scales=target[:, CODE_WORDS:SET_WORDS].bitcast(U8),
+                in_=qk_tiles[ft, g][:].rearrange("p w h n -> p (w h n)"),
             )
-            nc.vector.quantize_mx(
-                out=code_set["k_codes"][:, g, :].bitcast(FP8X4),
-                scales=code_set["k_scales"][:, g, :],
-                in_=k_bf[:].rearrange("p h n -> p (h n)"),
-            )
-            if g % BATCH == BATCH - 1:
-                groups = slice(g + 1 - BATCH, g + 1)
-                nc.sync.dma_start(
-                    out=code_set["q_scales_head0"][0:HALF, groups, :].bitcast(I32),
-                    in_=code_set["q_scales"][0:HALF, groups, :].bitcast(I32),
-                )
-                nc.sync.dma_start(
-                    out=code_set["q_scales_head1"][HALF:P, groups, :].bitcast(I32),
-                    in_=code_set["q_scales"][HALF:P, groups, :].bitcast(I32),
-                )
+            if unsorted:
+                for head in range(2):
+                    rows = slice(HALF * head, HALF * head + HALF)
+                    (nc.vector if place == UNSORTED_GROUPS - 1 else nc.gpsimd).tensor_copy(
+                        out=last_split[place][head][rows, :].bitcast(I32),
+                        in_=target[rows, CODE_WORDS : CODE_WORDS + COLS // PACK].bitcast(I32),
+                    )
+            elif member == 0:
+                nc.sync.dma_start(out=second[0:HALF, :].bitcast(I32), in_=first[HALF:P, :].bitcast(I32))
+            else:
+                nc.sync.dma_start(out=first[HALF:P, :].bitcast(I32), in_=target[0:HALF, :].bitcast(I32))
+                nc.gpsimd.tensor_copy(out=second[HALF:P, :].bitcast(I32), in_=target[HALF:P, :].bitcast(I32))
 
-        def logits_piece(ft, v):
-            code_set = code_sets[ft % CODE_SETS]
-            batch, n = v // LOGIT_GROUPS, v % LOGIT_GROUPS
-            i_tile, head = n // 2, n % 2
-            queries = slice(P * i_tile, P * i_tile + P)
-            if batch == 0:
-                accs[n] = bank(RING_BESIDE_LOGITS + n)
-            for g in range(BATCH * batch, BATCH * batch + BATCH):
+        def logits_pass(ft, i_tile, head, pair, acc):
+            codes = sorted_sets[ft % SETS][pair][head]
+            scale_words = P // PACK
+            nc.tensor.matmul_mx(
+                out=acc,
+                lhsT=codes[:, P * i_tile : P * i_tile + P].bitcast(FP8X4),
+                lhsT_scale=codes[:, CODE_WORDS + scale_words * i_tile : CODE_WORDS + scale_words * (i_tile + 1)].bitcast(U8),
+                rhs=codes[:, COLS : 2 * COLS].bitcast(FP8X4),
+                rhs_scale=codes[:, CODE_WORDS + COLS // PACK : SET_WORDS].bitcast(U8),
+                start=(pair == 0),
+                stop=(pair == PAIRS - 1),
+            )
+
+        def logits_piece(ft, piece):
+            i_tile, head, part = piece // 4, piece // 2 % 2, piece % 2
+            if piece % 4 == 0:
+                accs[ft, i_tile] = bank(6 + i_tile)
+            for pair in range(2 * part, 2 * part + 2):
+                logits_pass(ft, i_tile, head, pair, accs[ft, i_tile][:, COLS * head : COLS * head + COLS])
+
+        def tail_passes(kind, index):
+            last = FEATURE_TILES - 1
+            for n in range(4):
+                i_tile, head = n // 2, n % 2
+                if kind == "pair":
+                    if index == 0:
+                        accs[last, n] = bank(4 + n)
+                    logits_pass(last, i_tile, head, index, accs[last, n][:, 0:COLS])
+                    continue
+                codes = last_codes[index]
                 nc.tensor.matmul_mx(
-                    out=accs[n][:, 0:COLS],
-                    lhsT=code_set["q_codes"][:, g, queries].bitcast(FP8X4),
-                    lhsT_scale=code_set["q_scales_head%d" % head][:, g, queries],
-                    rhs=code_set["k_codes"][:, g, :].bitcast(FP8X4),
-                    rhs_scale=code_set["k_scales"][:, g, :],
-                    start=(g == 0),
-                    stop=(g == ROW_GROUPS - 1),
+                    out=accs[last, n][:, 0:COLS],
+                    lhsT=codes[:, P * i_tile : P * i_tile + P].bitcast(FP8X4),
+                    lhsT_scale=last_split[index][head][:, P * i_tile : P * i_tile + P],
+                    rhs=codes[:, COLS : 2 * COLS].bitcast(FP8X4),
+                    rhs_scale=codes[:, CODE_WORDS + COLS // PACK : SET_WORDS].bitcast(U8),
+                    start=False,
+                    stop=(index == UNSORTED_GROUPS - 1),
                 )
 
-        def store_logits(ft, n):
-            i_tile, head = n // 2, n % 2
-            result = out_pool.tile([P, COLS], F32, name="result")
-            nc.scalar.copy(out=result[:], in_=accs[n][:, 0:COLS])
-            nc.sync.dma_start(out=out[2 * ft + head, P * i_tile : P * i_tile + P, :], in_=result[:])
+        def store_logits(ft, i_tile):
+            result = out_pool.tile([P, 2, COLS], F32, name="result")
+            nc.scalar.copy(out=result[:].rearrange("p h j -> p (h j)"), in_=accs[ft, i_tile][:])
+            nc.sync.dma_start(
+                out=out[2 * ft : 2 * ft + 2, P * i_tile : P * i_tile + P, :].rearrange("h i j -> i h j"),
+                in_=result[:],
+            )
 
-        for t in range(2, X_LOADS_AHEAD):
-            load_x(t)
+        spread_mask(0)
+        copy_mask(0, True)
+        spread_mask(1)
+        copy_mask(1, False)
         transpose_x(0)
         bias_bank = psum.tile([P, P], BF16, name="bias_bank", tag="bank7")
         nc.tensor.transpose(out=bias_bank[:], in_=bias_rows[:], identity=ident_bf[:])
-        transpose_x(1)
-        w_grouped = []
-        for which in range(2):
-            grouped = weights.tile([P, EMBED, PACK], BF16, name="w_grouped", align_bytes=64)
-            nc.vector.tensor_copy(out=grouped[:], in_=w_raw[which][:].rearrange("p t c -> p c t"))
-            w_grouped.append(grouped)
-        for which in range(2):
-            nc.vector.quantize_mx(
-                out=w_codes[:, which, :].bitcast(FP8X4),
-                scales=w_scales[:, which, :],
-                in_=w_grouped[which][:].rearrange("p c t -> p (c t)"),
-            )
+        spread_mask(2)
+        copy_mask(2, False)
+        evacuate_x(0, 0)
+        evacuate_x(0, 1)
+        spread_mask(3)
+        copy_mask(3, False)
         nc.vector.tensor_copy(out=bias_cols[:], in_=bias_bank[:, 0 : 2 * FEATURE_TILES])
-        for t in range(2):
-            evacuate_x(t)
-            quantise_x(t)
-        project(0)
+        nc.vector.tensor_scalar(
+            out=bias_q_scaled[:], in0=bias_cols[:, 0:FEATURE_TILES], scalar1=SCALING, scalar2=None, op0=MULT
+        )
+        prepare_weights(0)
+        quantise_x(0)
+        transpose_x(1)
+        project(0, 0)
+        evacuate_x(1, 0)
+        evacuate_x(1, 1)
+        prepare_weights(1)
+        order = [(ft, t) for ft in range(FEATURE_TILES) for t in range(X_UNITS)]
 
-        for u in range(UNITS):
-            ft, v = u // UNITS_PER_TILE, u % UNITS_PER_TILE
-            if u + X_LOADS_AHEAD < UNITS_PER_TILE:
-                load_x(u + X_LOADS_AHEAD)
-            if u + 2 < UNITS_PER_TILE:
-                transpose_x(u + 2)
-            if u + 1 < UNITS:
-                project(u + 1)
-            if ft > 0:
-                logits_piece(ft - 1, v)
-            finish(u)
-            if u >= COL_HALVES and u % COL_HALVES == 0:
-                done = u // COL_HALVES - 1
-                quantise_qk(done // ROW_GROUPS, done % ROW_GROUPS)
-            if u + 2 < UNITS_PER_TILE:
-                evacuate_x(u + 2)
-                quantise_x(u + 2)
-            if ft > 0 and v // LOGIT_GROUPS == BATCHES - 1:
-                store_logits(ft - 1, v % LOGIT_GROUPS)
+        pieces = []
+        tail_pairs = []
+        to_mask = []
+        to_quantise = []
+        for slot, (ft, t) in enumerate(order):
+            streaming = ft == 0
+            if streaming and t + X_LOADS_AHEAD < X_UNITS:
+                load_x(t + X_LOADS_AHEAD)
+            if streaming and t + PREP_AHEAD < X_UNITS:
+                transpose_x(t + PREP_AHEAD)
+            if streaming and t + HEAD_MASKS < X_UNITS:
+                spread_mask(t + HEAD_MASKS)
+            if slot + 1 < X_UNITS:
+                quantise_x(slot + 1)
+                project(*order[slot + 1])
+            stores = []
+            if pieces and slot >= pieces[0][0]:
+                for repeat in range(1 if ft < FEATURE_TILES - 1 else 2):
+                    if pieces:
+                        ready, lft, piece = pieces.pop(0)
+                        logits_piece(lft, piece)
+                        if piece % 4 == 3:
+                            stores.append((lft, piece // 4))
+            elif not pieces and tail_pairs and slot >= tail_pairs[0][0]:
+                tail_passes(*tail_pairs.pop(0)[1:])
+            if X_UNITS <= slot + 1 < len(order):
+                project(*order[slot + 1])
+            finish(ft, t)
+            while to_mask and to_mask[0][0] <= slot:
+                when, mft, g = to_mask.pop(0)
+                mask_q(mft, g)
+            while to_quantise and to_quantise[0][0] <= slot:
+                when, qft, g = to_quantise.pop(0)
+                quantise_qk(qft, g)
+                if qft == FEATURE_TILES - 1:
+                    if g >= ROW_GROUPS - UNSORTED_GROUPS:
+                        tail_pairs.append((slot + 2, "group", g - (ROW_GROUPS - UNSORTED_GROUPS)))
+                    elif g % 2 == 1:
+                        tail_pairs.append((slot + SORT_LAG, "pair", g // 2))
+                elif g == ROW_GROUPS - 1:
+                    for piece in range(8):
+                        pieces.append((slot + SORT_LAG, qft, piece))
+            if t % COL_HALVES == COL_HALVES - 1:
+                g = t // COL_HALVES
+                if ft > 0 and g in SPLIT_GROUPS:
+                    to_mask.append((slot + 1, ft, g))
+                    to_quantise.append((slot + 1 + 1, ft, g))
+                else:
+                    to_quantise.append((slot + 1, ft, g))
+            if streaming and t + PREP_AHEAD < X_UNITS:
+                evacuate_x(t + PREP_AHEAD, 0)
+                evacuate_x(t + PREP_AHEAD, 1)
+            if streaming and t + HEAD_MASKS < X_UNITS:
+                copy_mask(t + HEAD_MASKS, t % 2 == 0)
+            for first, start in ((2, 18), (3, 34)):
+                if start <= slot < start + 2:
+                    interleave_weights(first, slot - start, nc.scalar.copy)
+                if slot == start + 4:
+                    quantise_weights(first)
+            if X_UNITS - 2 <= slot < X_UNITS - 2 + len(SPLIT_GROUPS):
+                make_keep_ones(slot - (X_UNITS - 2))
+            for item in stores:
+                store_logits(*item)
 
         quantise_qk(FEATURE_TILES - 1, ROW_GROUPS - 1)
-        for v in range(UNITS_PER_TILE):
-            logits_piece(FEATURE_TILES - 1, v)
-            if v // LOGIT_GROUPS == BATCHES - 1:
-                store_logits(FEATURE_TILES - 1, v % LOGIT_GROUPS)
+        last = FEATURE_TILES - 1
+        tail_pairs.append((0, "group", UNSORTED_GROUPS - 1))
+        for item in tail_pairs:
+            tail_passes(*item[1:])
+        for n in range(4):
+            i_tile, head = n // 2, n % 2
+            result = out_pool.tile([P, COLS], F32, name="last_result_%d" % head)
+            if head == 0:
+                nc.scalar.copy(out=result[:], in_=accs[last, n][:, 0:COLS])
+            else:
+                nc.vector.tensor_copy(out=result[:], in_=accs[last, n][:, 0:COLS])
+            nc.sync.dma_start(out=out[2 * last + head, P * i_tile : P * i_tile + P, :], in_=result[:])

@@ -31,13 +31,13 @@ UNSORTED_GROUPS = 4
 FIRST_TILES = 1
 STAGES = 3
 SPLIT_GROUPS = (3,)
-HEAD_MASKS = 4
+HEAD_MASKS = 6
 SETS = 2
 CODE_WORDS = 2 * COLS
 SET_WORDS = CODE_WORDS + CODE_WORDS // PACK
 X_LOADS_AHEAD = 6
-PREP_AHEAD = 2
-SORT_LAG = 8
+PREP_AHEAD = 3
+SORT_LAG = 10
 
 FLOPS = 2 * ROWS * COLS * EMBED * 2 * EMBED + 2 * HEADS * COLS * COLS * ROWS * HEAD_DIM
 
@@ -152,6 +152,7 @@ def tile_rowselfattention_pa_t_kernel(tc, x, mask, Wq, bq, Wk, bk, out):
         mask_views = {}
         qk_tiles = {}
         stages_taken = {}
+        late_moves = []
         accs = {}
 
         def transpose_x(t):
@@ -332,9 +333,17 @@ def tile_rowselfattention_pa_t_kernel(tc, x, mask, Wq, bq, Wk, bk, out):
                     )
             elif member == 0:
                 nc.sync.dma_start(out=second[0:HALF, :].bitcast(I32), in_=first[HALF:P, :].bitcast(I32))
+                flush_moves()
             else:
-                nc.sync.dma_start(out=first[HALF:P, :].bitcast(I32), in_=target[0:HALF, :].bitcast(I32))
                 nc.gpsimd.tensor_copy(out=second[HALF:P, :].bitcast(I32), in_=target[HALF:P, :].bitcast(I32))
+                late_moves.append((first, target))
+            if unsorted:
+                flush_moves()
+
+        def flush_moves():
+            while late_moves:
+                first, stage = late_moves.pop(0)
+                nc.sync.dma_start(out=first[HALF:P, :].bitcast(I32), in_=stage[0:HALF, :].bitcast(I32))
 
         def logits_pass(ft, i_tile, head, pair, acc):
             codes = sorted_sets[ft % SETS][pair][head]
@@ -366,13 +375,15 @@ def tile_rowselfattention_pa_t_kernel(tc, x, mask, Wq, bq, Wk, bk, out):
                     logits_pass(last, i_tile, head, index, accs[last, n][:, 0:COLS])
                     continue
                 codes = last_codes[index]
+                if index == 0 and UNSORTED_GROUPS == ROW_GROUPS:
+                    accs[last, n] = bank(4 + n)
                 nc.tensor.matmul_mx(
                     out=accs[last, n][:, 0:COLS],
                     lhsT=codes[:, P * i_tile : P * i_tile + P].bitcast(FP8X4),
                     lhsT_scale=last_split[index][head][:, P * i_tile : P * i_tile + P],
                     rhs=codes[:, COLS : 2 * COLS].bitcast(FP8X4),
                     rhs_scale=codes[:, CODE_WORDS + COLS // PACK : SET_WORDS].bitcast(U8),
-                    start=False,
+                    start=(index == 0 and UNSORTED_GROUPS == ROW_GROUPS),
                     stop=(index == UNSORTED_GROUPS - 1),
                 )
 
@@ -391,22 +402,29 @@ def tile_rowselfattention_pa_t_kernel(tc, x, mask, Wq, bq, Wk, bk, out):
         transpose_x(0)
         bias_bank = psum.tile([P, P], BF16, name="bias_bank", tag="bank7")
         nc.tensor.transpose(out=bias_bank[:], in_=bias_rows[:], identity=ident_bf[:])
-        spread_mask(2)
-        copy_mask(2, False)
         evacuate_x(0, 0)
         evacuate_x(0, 1)
-        spread_mask(3)
-        copy_mask(3, False)
+        spread_mask(2)
+        copy_mask(2, False)
         nc.vector.tensor_copy(out=bias_cols[:], in_=bias_bank[:, 0 : 2 * FEATURE_TILES])
         nc.vector.tensor_scalar(
             out=bias_q_scaled[:], in0=bias_cols[:, 0:FEATURE_TILES], scalar1=SCALING, scalar2=None, op0=MULT
         )
+        spread_mask(3)
+        copy_mask(3, True)
+        spread_mask(4)
+        copy_mask(4, True)
+        spread_mask(5)
+        copy_mask(5, True)
         prepare_weights(0)
         quantise_x(0)
         transpose_x(1)
         project(0, 0)
         evacuate_x(1, 0)
         evacuate_x(1, 1)
+        transpose_x(2)
+        evacuate_x(2, 0)
+        evacuate_x(2, 1)
         prepare_weights(1)
         order = [(ft, t) for ft in range(FEATURE_TILES) for t in range(X_UNITS)]
 

@@ -335,15 +335,15 @@ def tile_rowselfattention_pa_t_kernel(tc, x, mask, Wq, bq, Wk, bk, out):
                 nc.sync.dma_start(out=second[0:HALF, :].bitcast(I32), in_=first[HALF:P, :].bitcast(I32))
                 flush_moves()
             else:
-                nc.gpsimd.tensor_copy(out=second[HALF:P, :].bitcast(I32), in_=target[HALF:P, :].bitcast(I32))
-                late_moves.append((first, target))
+                late_moves.append((first, second, target))
             if unsorted:
                 flush_moves()
 
         def flush_moves():
             while late_moves:
-                first, stage = late_moves.pop(0)
+                first, second, stage = late_moves.pop(0)
                 nc.sync.dma_start(out=first[HALF:P, :].bitcast(I32), in_=stage[0:HALF, :].bitcast(I32))
+                nc.sync.dma_start(out=second[HALF:P, :].bitcast(I32), in_=stage[HALF:P, :].bitcast(I32))
 
         def logits_pass(ft, i_tile, head, pair, acc):
             codes = sorted_sets[ft % SETS][pair][head]

@@ -46,7 +46,6 @@ def tile_rowselfattention_pa_t_kernel(tc, x, mask, Wq, bq, Wk, bk, out):
     nc = tc.nc
     with ExitStack() as stack:
         const = stack.enter_context(tc.tile_pool(name="const", bufs=1))
-        weights = stack.enter_context(tc.tile_pool(name="weights", bufs=2))
         x_pool = stack.enter_context(tc.tile_pool(name="x_pool", bufs=X_LOADS_AHEAD))
         grouped_pool = stack.enter_context(tc.tile_pool(name="grouped_pool", bufs=3))
         qk_pool = stack.enter_context(tc.tile_pool(name="qk_pool", bufs=3))
@@ -92,15 +91,27 @@ def tile_rowselfattention_pa_t_kernel(tc, x, mask, Wq, bq, Wk, bk, out):
         nc.sync.dma_start(
             out=bias_rows[FEATURE_TILES : 2 * FEATURE_TILES, :], in_=bk.rearrange("(t p) -> t p", p=P)
         )
-        w_raw = []
+        w_first = []
+        w_rest = []
         for which, w in enumerate((Wq, Wk)):
-            raw = weights.tile([P, PACK, EMBED], BF16, name="w_raw")
-            nc.sync.dma_start(
-                out=raw[:].rearrange("p (u e) c -> p u (e c)", u=2),
-                in_=w.rearrange("(u q e) c -> q u (e c)", u=2, e=2),
-            )
-            w_raw.append(raw)
-        for t in range(1, X_LOADS_AHEAD):
+            raw = const.tile([P, PACK, P], BF16, name="w_first_%d" % which)
+            for u in range(2):
+                nc.sync.dma_start(
+                    out=raw[:, 2 * u : 2 * u + 2, :],
+                    in_=w[2 * P * u : 2 * P * u + 2 * P, 0:P].rearrange("(q e) c -> q e c", e=2),
+                )
+            w_first.append(raw)
+        for t in range(1, 6):
+            load_x(t)
+        for which, w in enumerate((Wq, Wk)):
+            raw = const.tile([P, PACK, EMBED - P], BF16, name="w_rest_%d" % which)
+            for u in range(2):
+                nc.sync.dma_start(
+                    out=raw[:, 2 * u : 2 * u + 2, :],
+                    in_=w[2 * P * u : 2 * P * u + 2 * P, P:EMBED].rearrange("(q e) c -> q e c", e=2),
+                )
+            w_rest.append(raw)
+        for t in range(6, X_LOADS_AHEAD):
             load_x(t)
 
         ident_f32 = const.tile([P, P], F32)
@@ -116,33 +127,20 @@ def tile_rowselfattention_pa_t_kernel(tc, x, mask, Wq, bq, Wk, bk, out):
         x_codes = const.tile([P, X_UNITS, TOKENS], U32, align_bytes=64)
         x_scales = const.tile([P, X_UNITS, TOKENS], U8, align_bytes=64)
         keep = const.tile([P, X_UNITS, TOKENS], F32)
-        stages = []
-        for s in range(STAGES):
-            stage = const.tile([P, SET_WORDS], U32, name="stage_%d" % s, align_bytes=64)
-            nc.gpsimd.memset(stage[:, CODE_WORDS:SET_WORDS].bitcast(I32), 0)
-            stages.append(stage)
-        sorted_sets = []
-        for s in range(SETS):
-            pairs = []
-            for pair in range(PAIRS):
-                tiles = [
-                    const.tile([P, SET_WORDS], U32, name="sorted_%d_%d_%d" % (s, pair, head), align_bytes=64)
-                    for head in range(2)
-                ]
-                nc.gpsimd.memset(tiles[0][:, CODE_WORDS:SET_WORDS].bitcast(I32), 0)
-                pairs.append(tiles)
-            sorted_sets.append(pairs)
-
-        last_codes = []
-        last_split = []
-        for m in range(UNSORTED_GROUPS):
-            codes = const.tile([P, SET_WORDS], U32, name="last_codes_%d" % m, align_bytes=64)
-            nc.gpsimd.memset(codes[:, CODE_WORDS:SET_WORDS].bitcast(I32), 0)
-            last_codes.append(codes)
-            planes = [const.tile([P, COLS], U8, name="last_split_%d_%d" % (m, head), align_bytes=64) for head in range(2)]
-            nc.gpsimd.memset(planes[0][HALF:P, :].bitcast(I32), 0)
-            nc.gpsimd.memset(planes[1][0:HALF, :].bitcast(I32), 0)
-            last_split.append(planes)
+        n_first = SETS * PAIRS
+        n_written = n_first + STAGES + UNSORTED_GROUPS
+        code_tiles = const.tile([P, n_written + n_first, SET_WORDS], U32, align_bytes=64)
+        nc.vector.memset(code_tiles[:, 0:n_written, CODE_WORDS:SET_WORDS].bitcast(I32), 0)
+        sorted_sets = [
+            [[code_tiles[:, PAIRS * s + pair, :], code_tiles[:, n_written + PAIRS * s + pair, :]] for pair in range(PAIRS)]
+            for s in range(SETS)
+        ]
+        stages = [code_tiles[:, n_first + s, :] for s in range(STAGES)]
+        last_codes = [code_tiles[:, n_first + STAGES + m, :] for m in range(UNSORTED_GROUPS)]
+        split_planes = const.tile([P, 2, UNSORTED_GROUPS, COLS], U8, align_bytes=64)
+        nc.vector.memset(split_planes[HALF:P, 0].bitcast(I32), 0)
+        nc.vector.memset(split_planes[0:HALF, 1].bitcast(I32), 0)
+        last_split = [[split_planes[:, head, m, :] for head in range(2)] for m in range(UNSORTED_GROUPS)]
 
         x_banks = {}
         grouped_tiles = {}
@@ -225,10 +223,11 @@ def tile_rowselfattention_pa_t_kernel(tc, x, mask, Wq, bq, Wk, bk, out):
         def interleave_weights(tile, which, copy):
             if which == 0:
                 grouped_weights[tile] = const.tile([P, 2, P, PACK], BF16, name="w_grouped_%d" % (tile % 2), align_bytes=64)
-            columns = slice(P * tile, P * tile + P)
-            copy(
-                out=grouped_weights[tile][:, which], in_=w_raw[which][:, :, columns].rearrange("p t c -> p c t")
-            )
+            if tile == 0:
+                raw = w_first[which][:]
+            else:
+                raw = w_rest[which][:, :, P * (tile - 1) : P * tile]
+            copy(out=grouped_weights[tile][:, which], in_=raw.rearrange("p t c -> p c t"))
 
         def quantise_weights(tile):
             nc.vector.quantize_mx(
@@ -404,20 +403,22 @@ def tile_rowselfattention_pa_t_kernel(tc, x, mask, Wq, bq, Wk, bk, out):
         nc.tensor.transpose(out=bias_bank[:], in_=bias_rows[:], identity=ident_bf[:])
         evacuate_x(0, 0)
         evacuate_x(0, 1)
-        spread_mask(2)
-        copy_mask(2, False)
         nc.vector.tensor_copy(out=bias_cols[:], in_=bias_bank[:, 0 : 2 * FEATURE_TILES])
         nc.vector.tensor_scalar(
             out=bias_q_scaled[:], in0=bias_cols[:, 0:FEATURE_TILES], scalar1=SCALING, scalar2=None, op0=MULT
         )
+        interleave_weights(0, 0, nc.vector.tensor_copy)
+        interleave_weights(0, 1, nc.vector.tensor_copy)
+        quantise_weights(0)
+        quantise_x(0)
+        spread_mask(2)
+        copy_mask(2, False)
         spread_mask(3)
         copy_mask(3, True)
         spread_mask(4)
         copy_mask(4, True)
         spread_mask(5)
         copy_mask(5, True)
-        prepare_weights(0)
-        quantise_x(0)
         transpose_x(1)
         project(0, 0)
         evacuate_x(1, 0)
@@ -425,7 +426,6 @@ def tile_rowselfattention_pa_t_kernel(tc, x, mask, Wq, bq, Wk, bk, out):
         transpose_x(2)
         evacuate_x(2, 0)
         evacuate_x(2, 1)
-        prepare_weights(1)
         order = [(ft, t) for ft in range(FEATURE_TILES) for t in range(X_UNITS)]
 
         pieces = []
@@ -482,9 +482,9 @@ def tile_rowselfattention_pa_t_kernel(tc, x, mask, Wq, bq, Wk, bk, out):
                 evacuate_x(t + PREP_AHEAD, 1)
             if streaming and t + HEAD_MASKS < X_UNITS:
                 copy_mask(t + HEAD_MASKS, t % 2 == 0)
-            for first, start in ((2, 18), (3, 34)):
+            for first, start, copy in ((1, 8, nc.vector.tensor_copy), (2, 18, nc.scalar.copy), (3, 34, nc.scalar.copy)):
                 if start <= slot < start + 2:
-                    interleave_weights(first, slot - start, nc.scalar.copy)
+                    interleave_weights(first, slot - start, copy)
                 if slot == start + 4:
                     quantise_weights(first)
             if X_UNITS - 2 <= slot < X_UNITS - 2 + len(SPLIT_GROUPS):

@@ -30,9 +30,17 @@ X_UNITS = ROW_GROUPS * COL_HALVES
 UNSORTED_GROUPS = 4
 FIRST_TILES = 1
 STAGES = 3
+VECTOR_EVACUATES = (0, 1, 2)
 SPLIT_GROUPS = (3,)
 HEAD_MASKS = 6
-SETS = 2
+SETS = 3
+LAG = 5
+MASK_SCALAR = (0, 2, 3, 4, 5, 7, 9, 11, 13, 15)
+W_STEPS = ((1, 2, "v"), (2, 24, "s"), (3, 38, "s"))
+ONES_SLOT = 28
+SPLIT_FROM = 2
+QK_BUFS = 4
+LATE = 9
 CODE_WORDS = 2 * COLS
 SET_WORDS = CODE_WORDS + CODE_WORDS // PACK
 X_LOADS_AHEAD = 6
@@ -48,7 +56,7 @@ def tile_rowselfattention_pa_t_kernel(tc, x, mask, Wq, bq, Wk, bk, out):
         const = stack.enter_context(tc.tile_pool(name="const", bufs=1))
         x_pool = stack.enter_context(tc.tile_pool(name="x_pool", bufs=X_LOADS_AHEAD))
         grouped_pool = stack.enter_context(tc.tile_pool(name="grouped_pool", bufs=3))
-        qk_pool = stack.enter_context(tc.tile_pool(name="qk_pool", bufs=3))
+        qk_pool = stack.enter_context(tc.tile_pool(name="qk_pool", bufs=QK_BUFS))
         raw_pool = stack.enter_context(tc.tile_pool(name="raw_pool", bufs=2))
         out_pool = stack.enter_context(tc.tile_pool(name="out_pool", bufs=2))
         psum = stack.enter_context(tc.psum_pool(name="psum", bufs=1))
@@ -65,19 +73,21 @@ def tile_rowselfattention_pa_t_kernel(tc, x, mask, Wq, bq, Wk, bk, out):
             return bank(index)
 
         def ring_of(ft, t):
-            if ft < FIRST_TILES:
+            if ft < 2:
                 return 8
-            return 6 if ft < FEATURE_TILES - 1 or t < 9 else 4
+            return 6 if ft < FEATURE_TILES - 1 or t < LATE else 4
 
         x_tiles = {}
 
         def load_x(t):
             g, half = t // COL_HALVES, t % COL_HALVES
             x_sb = x_pool.tile([P, PACK * EMBED], BF16, name="x_sb")
-            nc.sync.dma_start(
-                out=x_sb[:].rearrange("p (r e) -> p r e", r=PACK),
-                in_=x[PACK * g : PACK * g + PACK, P * half : P * half + P, :].rearrange("r p e -> p r e"),
-            )
+            rows = PACK
+            for r in range(0, PACK, rows):
+                nc.sync.dma_start(
+                    out=x_sb[:, r * EMBED : (r + rows) * EMBED].rearrange("p (r e) -> p r e", r=rows),
+                    in_=x[PACK * g + r : PACK * g + r + rows, P * half : P * half + P, :].rearrange("r p e -> p r e"),
+                )
             x_tiles[t] = x_sb
 
         bias_rows = const.tile([P, P], BF16)
@@ -87,10 +97,6 @@ def tile_rowselfattention_pa_t_kernel(tc, x, mask, Wq, bq, Wk, bk, out):
         nc.vector.memset(mask_rows[HALF:P, :], 0.0)
         nc.sync.dma_start(out=mask_rows[0:ROWS, :], in_=mask)
         load_x(0)
-        nc.sync.dma_start(out=bias_rows[0:FEATURE_TILES, :], in_=bq.rearrange("(t p) -> t p", p=P))
-        nc.sync.dma_start(
-            out=bias_rows[FEATURE_TILES : 2 * FEATURE_TILES, :], in_=bk.rearrange("(t p) -> t p", p=P)
-        )
         w_first = []
         w_rest = []
         for which, w in enumerate((Wq, Wk)):
@@ -101,7 +107,12 @@ def tile_rowselfattention_pa_t_kernel(tc, x, mask, Wq, bq, Wk, bk, out):
                     in_=w[2 * P * u : 2 * P * u + 2 * P, 0:P].rearrange("(q e) c -> q e c", e=2),
                 )
             w_first.append(raw)
-        for t in range(1, 6):
+        nc.sync.dma_start(out=bias_rows[0:FEATURE_TILES, :], in_=bq.rearrange("(t p) -> t p", p=P))
+        nc.sync.dma_start(
+            out=bias_rows[FEATURE_TILES : 2 * FEATURE_TILES, :], in_=bk.rearrange("(t p) -> t p", p=P)
+        )
+        load_x(1)
+        for t in range(2, 6):
             load_x(t)
         for which, w in enumerate((Wq, Wk)):
             raw = const.tile([P, PACK, EMBED - P], BF16, name="w_rest_%d" % which)
@@ -123,7 +134,7 @@ def tile_rowselfattention_pa_t_kernel(tc, x, mask, Wq, bq, Wk, bk, out):
         w_scales = const.tile([P, FEATURE_TILES, 2, P], U8, align_bytes=64)
         bias_cols = const.tile([P, 2 * FEATURE_TILES], F32)
         bias_q_scaled = const.tile([P, FEATURE_TILES], F32)
-        keep_ones = const.tile([P, 1, COL_HALVES * TOKENS], BF16)
+        keep_ones = const.tile([P, max(1, len(SPLIT_GROUPS)), COL_HALVES * TOKENS], BF16)
         x_codes = const.tile([P, X_UNITS, TOKENS], U32, align_bytes=64)
         x_scales = const.tile([P, X_UNITS, TOKENS], U8, align_bytes=64)
         keep = const.tile([P, X_UNITS, TOKENS], F32)
@@ -168,6 +179,8 @@ def tile_rowselfattention_pa_t_kernel(tc, x, mask, Wq, bq, Wk, bk, out):
                         )
                 pair_banks.append(x_view)
             x_banks[t] = pair_banks
+            if t + X_LOADS_AHEAD < X_UNITS:
+                load_x(t + X_LOADS_AHEAD)
 
         def spread_mask(t):
             g, half = t // COL_HALVES, t % COL_HALVES
@@ -189,7 +202,8 @@ def tile_rowselfattention_pa_t_kernel(tc, x, mask, Wq, bq, Wk, bk, out):
             if pair == 0:
                 grouped_tiles[t] = grouped_pool.tile([P, TOKENS * PACK], BF16, name="x_grouped", align_bytes=64)
             grouped_words = grouped_tiles[t][:].bitcast(F32).rearrange("p (i r u) -> p i r u", r=PACK, u=2)
-            nc.scalar.copy(
+            copy = nc.vector.tensor_copy if pair == 1 and t in VECTOR_EVACUATES else nc.scalar.copy
+            copy(
                 out=grouped_words[:, :, 2 * pair : 2 * pair + 2, :],
                 in_=pair_banks[pair].rearrange("p r u i -> p i r u"),
             )
@@ -261,10 +275,10 @@ def tile_rowselfattention_pa_t_kernel(tc, x, mask, Wq, bq, Wk, bk, out):
         def finish(ft, t):
             g, half = t // COL_HALVES, t % COL_HALVES
             if half == 0:
-                qk_tiles[ft, g] = qk_pool.tile([P, 2, COL_HALVES, TOKENS], BF16, name="qk_bf_%d" % (ft % FIRST_TILES), align_bytes=64)
+                qk_tiles[ft, g] = qk_pool.tile([P, 2, COL_HALVES, TOKENS], BF16, name="qk_bf", align_bytes=64)
             qk_bf = qk_tiles[ft, g]
             q_bank, k_bank = proj_banks[ft, t]
-            if ft > 0 and g in SPLIT_GROUPS:
+            if ft >= SPLIT_FROM and g in SPLIT_GROUPS:
                 if half == 0:
                     q_raw_tiles[ft, g] = raw_pool.tile([P, COL_HALVES, TOKENS], BF16, name="q_raw", align_bytes=64)
                 nc.scalar.activation(
@@ -398,35 +412,44 @@ def tile_rowselfattention_pa_t_kernel(tc, x, mask, Wq, bq, Wk, bk, out):
         copy_mask(0, True)
         spread_mask(1)
         copy_mask(1, False)
+        spread_mask(2)
+        copy_mask(2, True)
         transpose_x(0)
-        bias_bank = psum.tile([P, P], BF16, name="bias_bank", tag="bank7")
-        nc.tensor.transpose(out=bias_bank[:], in_=bias_rows[:], identity=ident_bf[:])
-        evacuate_x(0, 0)
-        evacuate_x(0, 1)
-        nc.vector.tensor_copy(out=bias_cols[:], in_=bias_bank[:, 0 : 2 * FEATURE_TILES])
-        nc.vector.tensor_scalar(
-            out=bias_q_scaled[:], in0=bias_cols[:, 0:FEATURE_TILES], scalar1=SCALING, scalar2=None, op0=MULT
-        )
         interleave_weights(0, 0, nc.vector.tensor_copy)
         interleave_weights(0, 1, nc.vector.tensor_copy)
+        evacuate_x(0, 0)
+        evacuate_x(0, 1)
         quantise_weights(0)
         quantise_x(0)
-        spread_mask(2)
-        copy_mask(2, False)
         spread_mask(3)
         copy_mask(3, True)
         spread_mask(4)
         copy_mask(4, True)
-        spread_mask(5)
-        copy_mask(5, True)
+        bias_index = banks_taken[0] % 8
+        banks_taken[0] += 1
+        bias_bank = psum.tile([P, P], BF16, name="bias_bank", tag="bank%d" % bias_index)
+        nc.tensor.transpose(out=bias_bank[:], in_=bias_rows[:], identity=ident_bf[:])
+        nc.vector.tensor_copy(out=bias_cols[:], in_=bias_bank[:, 0 : 2 * FEATURE_TILES])
+        nc.vector.tensor_scalar(
+            out=bias_q_scaled[:], in0=bias_cols[:, 0:FEATURE_TILES], scalar1=SCALING, scalar2=None, op0=MULT
+        )
         transpose_x(1)
-        project(0, 0)
         evacuate_x(1, 0)
         evacuate_x(1, 1)
+        project(0, 0)
         transpose_x(2)
+        quantise_x(1)
+        spread_mask(5)
         evacuate_x(2, 0)
         evacuate_x(2, 1)
-        order = [(ft, t) for ft in range(FEATURE_TILES) for t in range(X_UNITS)]
+        copy_mask(5, True)
+        order = []
+        for t in range(X_UNITS + LAG):
+            if t < X_UNITS:
+                order.append((0, t))
+            if t >= LAG:
+                order.append((1, t - LAG))
+        order += [(ft, t) for ft in (2, 3) for t in range(X_UNITS)]
 
         pieces = []
         tail_pairs = []
@@ -434,14 +457,15 @@ def tile_rowselfattention_pa_t_kernel(tc, x, mask, Wq, bq, Wk, bk, out):
         to_quantise = []
         for slot, (ft, t) in enumerate(order):
             streaming = ft == 0
-            if streaming and t + X_LOADS_AHEAD < X_UNITS:
-                load_x(t + X_LOADS_AHEAD)
             if streaming and t + PREP_AHEAD < X_UNITS:
                 transpose_x(t + PREP_AHEAD)
             if streaming and t + HEAD_MASKS < X_UNITS:
                 spread_mask(t + HEAD_MASKS)
-            if slot + 1 < X_UNITS:
-                quantise_x(slot + 1)
+            if slot < 2 * X_UNITS:
+                finish(ft, t)
+                if streaming and t + 2 < X_UNITS:
+                    quantise_x(t + 2)
+            if slot + 1 < 2 * X_UNITS:
                 project(*order[slot + 1])
             stores = []
             if pieces and slot >= pieces[0][0]:
@@ -453,9 +477,10 @@ def tile_rowselfattention_pa_t_kernel(tc, x, mask, Wq, bq, Wk, bk, out):
                             stores.append((lft, piece // 4))
             elif not pieces and tail_pairs and slot >= tail_pairs[0][0]:
                 tail_passes(*tail_pairs.pop(0)[1:])
-            if X_UNITS <= slot + 1 < len(order):
+            if 2 * X_UNITS <= slot + 1 < len(order):
                 project(*order[slot + 1])
-            finish(ft, t)
+            if slot >= 2 * X_UNITS:
+                finish(ft, t)
             while to_mask and to_mask[0][0] <= slot:
                 when, mft, g = to_mask.pop(0)
                 mask_q(mft, g)
@@ -472,7 +497,7 @@ def tile_rowselfattention_pa_t_kernel(tc, x, mask, Wq, bq, Wk, bk, out):
                         pieces.append((slot + SORT_LAG, qft, piece))
             if t % COL_HALVES == COL_HALVES - 1:
                 g = t // COL_HALVES
-                if ft > 0 and g in SPLIT_GROUPS:
+                if ft >= SPLIT_FROM and g in SPLIT_GROUPS:
                     to_mask.append((slot + 1, ft, g))
                     to_quantise.append((slot + 1 + 1, ft, g))
                 else:
@@ -481,14 +506,15 @@ def tile_rowselfattention_pa_t_kernel(tc, x, mask, Wq, bq, Wk, bk, out):
                 evacuate_x(t + PREP_AHEAD, 0)
                 evacuate_x(t + PREP_AHEAD, 1)
             if streaming and t + HEAD_MASKS < X_UNITS:
-                copy_mask(t + HEAD_MASKS, t % 2 == 0)
-            for first, start, copy in ((1, 8, nc.vector.tensor_copy), (2, 18, nc.scalar.copy), (3, 34, nc.scalar.copy)):
+                copy_mask(t + HEAD_MASKS, t + HEAD_MASKS in MASK_SCALAR)
+            for first, start, which_engine in W_STEPS:
+                copy = {"v": nc.vector.tensor_copy, "s": nc.scalar.copy}[which_engine]
                 if start <= slot < start + 2:
                     interleave_weights(first, slot - start, copy)
-                if slot == start + 4:
+                if slot == start + (2 if first == 1 else 4):
                     quantise_weights(first)
-            if X_UNITS - 2 <= slot < X_UNITS - 2 + len(SPLIT_GROUPS):
-                make_keep_ones(slot - (X_UNITS - 2))
+            if ONES_SLOT <= slot < ONES_SLOT + len(SPLIT_GROUPS):
+                make_keep_ones(slot - ONES_SLOT)
             for item in stores:
                 store_logits(*item)
 

@@ -30,6 +30,7 @@ X_UNITS = ROW_GROUPS * COL_HALVES
 UNSORTED_GROUPS = 4
 FIRST_TILES = 1
 STAGES = 3
+GP_WEIGHTS = (1, 2, 3)
 VECTOR_EVACUATES = (0, 1, 2)
 SPLIT_GROUPS = (3,)
 HEAD_MASKS = 6
@@ -40,7 +41,7 @@ W_STEPS = ((1, 2, "v"), (2, 24, "s"), (3, 38, "s"))
 ONES_SLOT = 28
 SPLIT_FROM = 2
 QK_BUFS = 4
-LATE = 9
+LATE = 13
 CODE_WORDS = 2 * COLS
 SET_WORDS = CODE_WORDS + CODE_WORDS // PACK
 X_LOADS_AHEAD = 6
@@ -241,6 +242,16 @@ def tile_rowselfattention_pa_t_kernel(tc, x, mask, Wq, bq, Wk, bk, out):
                 raw = w_first[which][:]
             else:
                 raw = w_rest[which][:, :, P * (tile - 1) : P * tile]
+            if tile in GP_WEIGHTS:
+                nc.gpsimd.tensor_scalar(
+                    out=grouped_weights[tile][:, which],
+                    in0=raw.rearrange("p t c -> p c t"),
+                    scalar1=1.0,
+                    scalar2=0.0,
+                    op0=MULT,
+                    op1=ADD,
+                )
+                return
             copy(out=grouped_weights[tile][:, which], in_=raw.rearrange("p t c -> p c t"))
 
         def quantise_weights(tile):
@@ -332,11 +343,20 @@ def tile_rowselfattention_pa_t_kernel(tc, x, mask, Wq, bq, Wk, bk, out):
             unsorted = ft == FEATURE_TILES - 1 and place >= 0
             if unsorted:
                 target = last_codes[place]
-            nc.vector.quantize_mx(
-                out=target[:, 0:CODE_WORDS].bitcast(FP8X4),
-                scales=target[:, CODE_WORDS:SET_WORDS].bitcast(U8),
-                in_=qk_tiles[ft, g][:].rearrange("p w h n -> p (w h n)"),
-            )
+            apart = unsorted and place == UNSORTED_GROUPS - 1
+            for which in range(2) if apart else (slice(0, 2),):
+                words = slice(COLS * which, COLS * which + COLS) if apart else slice(0, CODE_WORDS)
+                bytes_as_words = (
+                    slice(CODE_WORDS + COLS // PACK * which, CODE_WORDS + COLS // PACK * (which + 1))
+                    if apart
+                    else slice(CODE_WORDS, SET_WORDS)
+                )
+                values = qk_tiles[ft, g][:, which]
+                nc.vector.quantize_mx(
+                    out=target[:, words].bitcast(FP8X4),
+                    scales=target[:, bytes_as_words].bitcast(U8),
+                    in_=values.rearrange("p h n -> p (h n)") if apart else values.rearrange("p w h n -> p (w h n)"),
+                )
             if unsorted:
                 for head in range(2):
                     rows = slice(HALF * head, HALF * head + HALF)

@@ -108,11 +108,11 @@ def tile_rowselfattention_pa_t_kernel(tc, x, mask, Wq, bq, Wk, bk, out):
                     in_=w[2 * P * u : 2 * P * u + 2 * P, 0:P].rearrange("(q e) c -> q e c", e=2),
                 )
             w_first.append(raw)
+        load_x(1)
         nc.sync.dma_start(out=bias_rows[0:FEATURE_TILES, :], in_=bq.rearrange("(t p) -> t p", p=P))
         nc.sync.dma_start(
             out=bias_rows[FEATURE_TILES : 2 * FEATURE_TILES, :], in_=bk.rearrange("(t p) -> t p", p=P)
         )
-        load_x(1)
         for t in range(2, 6):
             load_x(t)
         for which, w in enumerate((Wq, Wk)):
@@ -443,26 +443,27 @@ def tile_rowselfattention_pa_t_kernel(tc, x, mask, Wq, bq, Wk, bk, out):
         quantise_x(0)
         spread_mask(3)
         copy_mask(3, True)
-        spread_mask(4)
-        copy_mask(4, True)
+        transpose_x(1)
         bias_index = banks_taken[0] % 8
         banks_taken[0] += 1
         bias_bank = psum.tile([P, P], BF16, name="bias_bank", tag="bank%d" % bias_index)
         nc.tensor.transpose(out=bias_bank[:], in_=bias_rows[:], identity=ident_bf[:])
         nc.vector.tensor_copy(out=bias_cols[:], in_=bias_bank[:, 0 : 2 * FEATURE_TILES])
+        evacuate_x(1, 0)
+        evacuate_x(1, 1)
         nc.vector.tensor_scalar(
             out=bias_q_scaled[:], in0=bias_cols[:, 0:FEATURE_TILES], scalar1=SCALING, scalar2=None, op0=MULT
         )
-        transpose_x(1)
-        evacuate_x(1, 0)
-        evacuate_x(1, 1)
         project(0, 0)
+        finish(0, 0)
+        spread_mask(4)
+        copy_mask(4, True)
         transpose_x(2)
         quantise_x(1)
-        spread_mask(5)
         evacuate_x(2, 0)
         evacuate_x(2, 1)
-        copy_mask(5, True)
+        spread_mask(5)
+        copy_mask(5, False)
         order = []
         for t in range(X_UNITS + LAG):
             if t < X_UNITS:
@@ -482,7 +483,8 @@ def tile_rowselfattention_pa_t_kernel(tc, x, mask, Wq, bq, Wk, bk, out):
             if streaming and t + HEAD_MASKS < X_UNITS:
                 spread_mask(t + HEAD_MASKS)
             if slot < 2 * X_UNITS:
-                finish(ft, t)
+                if slot > 0:
+                    finish(ft, t)
                 if streaming and t + 2 < X_UNITS:
                     quantise_x(t + 2)
             if slot + 1 < 2 * X_UNITS:

@@ -131,17 +131,17 @@ def tile_rowselfattention_pa_t_kernel(tc, x, mask, Wq, bq, Wk, bk, out):
         ident_bf = const.tile([P, P], BF16)
         nc.vector.tensor_copy(out=ident_bf[:], in_=ident_f32[:])
 
-        w_codes = const.tile([P, FEATURE_TILES, 2, P], U32, align_bytes=64)
-        w_scales = const.tile([P, FEATURE_TILES, 2, P], U8, align_bytes=64)
+        w_codes = const.tile([P, FEATURE_TILES, 2, P], U32, align_bytes=256)
+        w_scales = const.tile([P, FEATURE_TILES, 2, P], U8, align_bytes=256)
         bias_cols = const.tile([P, 2 * FEATURE_TILES], F32)
         bias_q_scaled = const.tile([P, FEATURE_TILES], F32)
         keep_ones = const.tile([P, max(1, len(SPLIT_GROUPS)), COL_HALVES * TOKENS], BF16)
-        x_codes = const.tile([P, X_UNITS, TOKENS], U32, align_bytes=64)
-        x_scales = const.tile([P, X_UNITS, TOKENS], U8, align_bytes=64)
+        x_codes = const.tile([P, X_UNITS, TOKENS], U32, align_bytes=256)
+        x_scales = const.tile([P, X_UNITS, TOKENS], U8, align_bytes=256)
         keep = const.tile([P, X_UNITS, TOKENS], F32)
         n_first = SETS * PAIRS
         n_written = n_first + STAGES + UNSORTED_GROUPS
-        code_tiles = const.tile([P, n_written + n_first, SET_WORDS], U32, align_bytes=64)
+        code_tiles = const.tile([P, n_written + n_first, SET_WORDS], U32, align_bytes=256)
         nc.vector.memset(code_tiles[:, 0:n_written, CODE_WORDS:SET_WORDS].bitcast(I32), 0)
         sorted_sets = [
             [[code_tiles[:, PAIRS * s + pair, :], code_tiles[:, n_written + PAIRS * s + pair, :]] for pair in range(PAIRS)]
@@ -149,7 +149,7 @@ def tile_rowselfattention_pa_t_kernel(tc, x, mask, Wq, bq, Wk, bk, out):
         ]
         stages = [code_tiles[:, n_first + s, :] for s in range(STAGES)]
         last_codes = [code_tiles[:, n_first + STAGES + m, :] for m in range(UNSORTED_GROUPS)]
-        split_planes = const.tile([P, 2, UNSORTED_GROUPS, COLS], U8, align_bytes=64)
+        split_planes = const.tile([P, 2, UNSORTED_GROUPS, COLS], U8, align_bytes=256)
         nc.vector.memset(split_planes[HALF:P, 0].bitcast(I32), 0)
         nc.vector.memset(split_planes[0:HALF, 1].bitcast(I32), 0)
         last_split = [[split_planes[:, head, m, :] for head in range(2)] for m in range(UNSORTED_GROUPS)]

@@ -30,14 +30,14 @@ X_UNITS = ROW_GROUPS * COL_HALVES
 UNSORTED_GROUPS = 4
 FIRST_TILES = 1
 STAGES = 3
-GP_WEIGHTS = (1, 2, 3)
+GP_WEIGHTS = (1,)
 VECTOR_EVACUATES = (0, 1, 2)
 SPLIT_GROUPS = (3,)
 HEAD_MASKS = 6
 SETS = 3
 LAG = 5
 MASK_SCALAR = (0, 2, 3, 4, 5, 7, 9, 11, 13, 15)
-W_STEPS = ((1, 2, "v"), (2, 24, "s"), (3, 38, "s"))
+W_STEPS = ((1, 2, "v"), (2, 26, "s"), (3, 34, "s"))
 ONES_SLOT = 28
 SPLIT_FROM = 2
 QK_BUFS = 4

@@ -30,6 +30,8 @@ X_UNITS = ROW_GROUPS * COL_HALVES
 UNSORTED_GROUPS = 4
 FIRST_TILES = 1
 STAGES = 3
+WARM_FIRST = 12
+WARM_UNITS = {1: 8, 2: 4}
 GP_WEIGHTS = (1,)
 VECTOR_EVACUATES = (0, 1, 2)
 SPLIT_GROUPS = (3,)
@@ -37,7 +39,7 @@ HEAD_MASKS = 6
 SETS = 3
 LAG = 5
 MASK_SCALAR = (0, 2, 3, 4, 5, 7, 9, 11, 13, 15)
-W_STEPS = ((1, 2, "v"), (2, 26, "s"), (3, 34, "s"))
+W_STEPS = ((1, 1, 2, 3, "v"), (2, 26, 27, 28, "s"), (3, 34, 35, 38, "s"))
 ONES_SLOT = 28
 SPLIT_FROM = 2
 QK_BUFS = 4
@@ -64,11 +66,16 @@ def tile_rowselfattention_pa_t_kernel(tc, x, mask, Wq, bq, Wk, bk, out):
         stack.enter_context(tc.manual_schedule())
 
         banks_taken = [0]
+        ring_now = [8]
 
         def bank(index):
             return psum.tile([P, BANK], F32, name="bank%d" % index, tag="bank%d" % index)
 
         def next_bank(ring):
+            if ring < ring_now[0]:
+                following = banks_taken[0] % ring_now[0]
+                banks_taken[0] = following if following < ring else 0
+                ring_now[0] = ring
             index = banks_taken[0] % ring
             banks_taken[0] += 1
             return bank(index)
@@ -172,6 +179,9 @@ def tile_rowselfattention_pa_t_kernel(tc, x, mask, Wq, bq, Wk, bk, out):
             for pair in range(2):
                 x_bank = next_bank(8)
                 x_view = x_bank[:].rearrange("p (r u i) -> p r u i", r=2, u=2)
+                if pair == 0 and t in WARM_UNITS:
+                    for repeat in range(WARM_UNITS[t]):
+                        nc.tensor.matmul(out=x_bank[:, 0:P], lhsT=ident_bf[:], rhs=ident_bf[:], start=True, stop=True)
                 for r in range(2):
                     for u in range(2):
                         first = (2 * pair + r) * (EMBED // 2) + u * P
@@ -428,6 +438,13 @@ def tile_rowselfattention_pa_t_kernel(tc, x, mask, Wq, bq, Wk, bk, out):
                 in_=result[:],
             )
 
+        warm_bank = psum.tile([P, P], F32, name="warm_bank", tag="bank7")
+
+        def keep_warm(count, out):
+            for repeat in range(count):
+                nc.tensor.matmul(out=out, lhsT=ident_bf[:], rhs=ident_bf[:], start=True, stop=True)
+
+        keep_warm(WARM_FIRST, warm_bank[:])
         spread_mask(0)
         copy_mask(0, True)
         spread_mask(1)
@@ -529,11 +546,13 @@ def tile_rowselfattention_pa_t_kernel(tc, x, mask, Wq, bq, Wk, bk, out):
                 evacuate_x(t + PREP_AHEAD, 1)
             if streaming and t + HEAD_MASKS < X_UNITS:
                 copy_mask(t + HEAD_MASKS, t + HEAD_MASKS in MASK_SCALAR)
-            for first, start, which_engine in W_STEPS:
+            for first, first_slot, second_slot, quantise_slot, which_engine in W_STEPS:
                 copy = {"v": nc.vector.tensor_copy, "s": nc.scalar.copy}[which_engine]
-                if start <= slot < start + 2:
-                    interleave_weights(first, slot - start, copy)
-                if slot == start + (2 if first == 1 else 4):
+                if slot == first_slot:
+                    interleave_weights(first, 0, copy)
+                if slot == second_slot:
+                    interleave_weights(first, 1, copy)
+                if slot == quantise_slot:
                     quantise_weights(first)
             if ONES_SLOT <= slot < ONES_SLOT + len(SPLIT_GROUPS):
                 make_keep_ones(slot - ONES_SLOT)

from contextlib import ExitStack

import concourse.mybir as mybir
from concourse.masks import make_identity

F32 = mybir.dt.float32
BF16 = mybir.dt.bfloat16
U32 = mybir.dt.uint32
I32 = mybir.dt.int32
U8 = mybir.dt.uint8
FP8X4 = mybir.dt.float8_e4m3fn_x4
ADD = mybir.AluOpType.add
MULT = mybir.AluOpType.mult
ACT = mybir.ActivationFunctionType

ROWS, COLS, EMBED, HEADS = 32, 256, 512, 8
HEAD_DIM = EMBED // HEADS
SCALING = HEAD_DIM**-0.5 / ROWS**0.5

P = 128
PACK = 4
BANK = 512
ROW_GROUPS = ROWS // PACK
PAIRS = ROW_GROUPS // 2
COL_HALVES = COLS // P
FEATURE_TILES = EMBED // P
HALF = P // 2
TOKENS = P * PACK
X_UNITS = ROW_GROUPS * COL_HALVES
UNSORTED_GROUPS = 4
FIRST_TILES = 1
STAGES = 3
WARM_FIRST = 12
WARM_UNITS = {1: 8, 2: 4}
GP_WEIGHTS = (1,)
VECTOR_EVACUATES = (0, 1, 2)
SPLIT_GROUPS = (3,)
HEAD_MASKS = 6
SETS = 3
LAG = 5
MASK_SCALAR = (0, 2, 3, 4, 5, 7, 9, 11, 13, 15)
W_STEPS = ((1, 1, 2, 3, "v"), (2, 26, 27, 28, "s"), (3, 34, 35, 38, "s"))
ONES_SLOT = 28
SPLIT_FROM = 2
QK_BUFS = 4
LATE = 13
CODE_WORDS = 2 * COLS
SET_WORDS = CODE_WORDS + CODE_WORDS // PACK
X_LOADS_AHEAD = 6
PREP_AHEAD = 3
SORT_LAG = 10

FLOPS = 2 * ROWS * COLS * EMBED * 2 * EMBED + 2 * HEADS * COLS * COLS * ROWS * HEAD_DIM


def tile_rowselfattention_pa_t_kernel(tc, x, mask, Wq, bq, Wk, bk, out):
    nc = tc.nc
    with ExitStack() as stack:
        const = stack.enter_context(tc.tile_pool(name="const", bufs=1))
        x_pool = stack.enter_context(tc.tile_pool(name="x_pool", bufs=X_LOADS_AHEAD))
        grouped_pool = stack.enter_context(tc.tile_pool(name="grouped_pool", bufs=3))
        qk_pool = stack.enter_context(tc.tile_pool(name="qk_pool", bufs=QK_BUFS))
        raw_pool = stack.enter_context(tc.tile_pool(name="raw_pool", bufs=2))
        out_pool = stack.enter_context(tc.tile_pool(name="out_pool", bufs=2))
        psum = stack.enter_context(tc.psum_pool(name="psum", bufs=1))
        stack.enter_context(tc.manual_schedule())

        banks_taken = [0]
        ring_now = [8]

        def bank(index):
            return psum.tile([P, BANK], F32, name="bank%d" % index, tag="bank%d" % index)

        def next_bank(ring):
            if ring < ring_now[0]:
                following = banks_taken[0] % ring_now[0]
                banks_taken[0] = following if following < ring else 0
                ring_now[0] = ring
            index = banks_taken[0] % ring
            banks_taken[0] += 1
            return bank(index)

        def ring_of(ft, t):
            if ft < 2:
                return 8
            return 6 if ft < FEATURE_TILES - 1 or t < LATE else 4

        x_tiles = {}

        def load_x(t):
            g, half = t // COL_HALVES, t % COL_HALVES
            x_sb = x_pool.tile([P, PACK * EMBED], BF16, name="x_sb")
            rows = PACK
            for r in range(0, PACK, rows):
                nc.sync.dma_start(
                    out=x_sb[:, r * EMBED : (r + rows) * EMBED].rearrange("p (r e) -> p r e", r=rows),
                    in_=x[PACK * g + r : PACK * g + r + rows, P * half : P * half + P, :].rearrange("r p e -> p r e"),
                )
            x_tiles[t] = x_sb

        bias_rows = const.tile([P, P], BF16)
        mask_rows = const.tile([P, COLS], BF16)
        nc.vector.memset(bias_rows[:], 0.0)
        nc.vector.memset(mask_rows[ROWS : 2 * ROWS, :], 0.0)
        nc.vector.memset(mask_rows[HALF:P, :], 0.0)
        nc.sync.dma_start(out=mask_rows[0:ROWS, :], in_=mask)
        load_x(0)
        w_first = []
        w_rest = []
        for which, w in enumerate((Wq, Wk)):
            raw = const.tile([P, PACK, P], BF16, name="w_first_%d" % which)
            for u in range(2):
                nc.sync.dma_start(
                    out=raw[:, 2 * u : 2 * u + 2, :],
                    in_=w[2 * P * u : 2 * P * u + 2 * P, 0:P].rearrange("(q e) c -> q e c", e=2),
                )
            w_first.append(raw)
        load_x(1)
        nc.sync.dma_start(out=bias_rows[0:FEATURE_TILES, :], in_=bq.rearrange("(t p) -> t p", p=P))
        nc.sync.dma_start(
            out=bias_rows[FEATURE_TILES : 2 * FEATURE_TILES, :], in_=bk.rearrange("(t p) -> t p", p=P)
        )
        for t in range(2, 6):
            load_x(t)
        for which, w in enumerate((Wq, Wk)):
            raw = const.tile([P, PACK, EMBED - P], BF16, name="w_rest_%d" % which)
            for u in range(2):
                nc.sync.dma_start(
                    out=raw[:, 2 * u : 2 * u + 2, :],
                    in_=w[2 * P * u : 2 * P * u + 2 * P, P:EMBED].rearrange("(q e) c -> q e c", e=2),
                )
            w_rest.append(raw)
        for t in range(6, X_LOADS_AHEAD):
            load_x(t)

        ident_f32 = const.tile([P, P], F32)
        make_identity(nc, ident_f32[:])
        ident_bf = const.tile([P, P], BF16)
        nc.vector.tensor_copy(out=ident_bf[:], in_=ident_f32[:])

        w_codes = const.tile([P, FEATURE_TILES, 2, P], U32, align_bytes=256)
        w_scales = const.tile([P, FEATURE_TILES, 2, P], U8, align_bytes=256)
        bias_cols = const.tile([P, 2 * FEATURE_TILES], F32)
        bias_q_scaled = const.tile([P, FEATURE_TILES], F32)
        keep_ones = const.tile([P, max(1, len(SPLIT_GROUPS)), COL_HALVES * TOKENS], BF16)
        x_codes = const.tile([P, X_UNITS, TOKENS], U32, align_bytes=256)
        x_scales = const.tile([P, X_UNITS, TOKENS], U8, align_bytes=256)
        keep = const.tile([P, X_UNITS, TOKENS], F32)
        n_first = SETS * PAIRS
        n_written = n_first + STAGES + UNSORTED_GROUPS
        code_tiles = const.tile([P, n_written + n_first, SET_WORDS], U32, align_bytes=256)
        nc.vector.memset(code_tiles[:, 0:n_written, CODE_WORDS:SET_WORDS].bitcast(I32), 0)
        sorted_sets = [
            [[code_tiles[:, PAIRS * s + pair, :], code_tiles[:, n_written + PAIRS * s + pair, :]] for pair in range(PAIRS)]
            for s in range(SETS)
        ]
        stages = [code_tiles[:, n_first + s, :] for s in range(STAGES)]
        last_codes = [code_tiles[:, n_first + STAGES + m, :] for m in range(UNSORTED_GROUPS)]
        split_planes = const.tile([P, 2, UNSORTED_GROUPS, COLS], U8, align_bytes=256)
        nc.vector.memset(split_planes[HALF:P, 0].bitcast(I32), 0)
        nc.vector.memset(split_planes[0:HALF, 1].bitcast(I32), 0)
        last_split = [[split_planes[:, head, m, :] for head in range(2)] for m in range(UNSORTED_GROUPS)]

        x_banks = {}
        grouped_tiles = {}
        proj_banks = {}
        q_raw_tiles = {}
        grouped_weights = {}
        mask_views = {}
        qk_tiles = {}
        stages_taken = {}
        late_moves = []
        accs = {}

        def transpose_x(t):
            g, half = t // COL_HALVES, t % COL_HALVES
            x_words = x_tiles[t][:].bitcast(F32)
            pair_banks = []
            for pair in range(2):
                x_bank = next_bank(8)
                x_view = x_bank[:].rearrange("p (r u i) -> p r u i", r=2, u=2)
                if pair == 0 and t in WARM_UNITS:
                    for repeat in range(WARM_UNITS[t]):
                        nc.tensor.matmul(out=x_bank[:, 0:P], lhsT=ident_bf[:], rhs=ident_bf[:], start=True, stop=True)
                for r in range(2):
                    for u in range(2):
                        first = (2 * pair + r) * (EMBED // 2) + u * P
                        nc.tensor.transpose(
                            out=x_view[:, r, u, :], in_=x_words[:, first : first + P], identity=ident_f32[:]
                        )
                pair_banks.append(x_view)
            x_banks[t] = pair_banks
            if t + X_LOADS_AHEAD < X_UNITS:
                load_x(t + X_LOADS_AHEAD)

        def spread_mask(t):
            g, half = t // COL_HALVES, t % COL_HALVES
            mask_bank = next_bank(8)
            mask_view = mask_bank[:].rearrange("p (r i) -> p r i", r=PACK)
            for r in range(PACK):
                row = PACK * g + r
                nc.tensor.matmul(
                    out=mask_view[:, r, :],
                    lhsT=ident_bf[:, row : row + 1].to_broadcast([P, P]),
                    rhs=mask_rows[:, P * half : P * half + P],
                    start=True,
                    stop=True,
                )
            mask_views[t] = mask_view

        def evacuate_x(t, pair):
            pair_banks = x_banks[t]
            if pair == 0:
                grouped_tiles[t] = grouped_pool.tile([P, TOKENS * PACK], BF16, name="x_grouped", align_bytes=64)
            grouped_words = grouped_tiles[t][:].bitcast(F32).rearrange("p (i r u) -> p i r u", r=PACK, u=2)
            copy = nc.vector.tensor_copy if pair == 1 and t in VECTOR_EVACUATES else nc.scalar.copy
            copy(
                out=grouped_words[:, :, 2 * pair : 2 * pair + 2, :],
                in_=pair_banks[pair].rearrange("p r u i -> p i r u"),
            )

        def copy_mask(t, on_scalar):
            mask_view = mask_views[t]
            keep_view = keep[:, t, :].rearrange("p (i r) -> p i r", r=PACK)
            if on_scalar:
                nc.scalar.activation(
                    out=keep_view,
                    in_=mask_view.rearrange("p r i -> p i r"),
                    func=ACT.Copy,
                    scale=-SCALING,
                    bias=SCALING,
                )
            else:
                nc.vector.tensor_scalar(
                    out=keep_view,
                    in0=mask_view.rearrange("p r i -> p i r"),
                    scalar1=-SCALING,
                    scalar2=SCALING,
                    op0=MULT,
                    op1=ADD,
                )

        def quantise_x(t):
            nc.vector.quantize_mx(
                out=x_codes[:, t, :].bitcast(FP8X4), scales=x_scales[:, t, :], in_=grouped_tiles[t][:]
            )

        def interleave_weights(tile, which, copy):
            if which == 0:
                grouped_weights[tile] = const.tile([P, 2, P, PACK], BF16, name="w_grouped_%d" % (tile % 2), align_bytes=64)
            if tile == 0:
                raw = w_first[which][:]
            else:
                raw = w_rest[which][:, :, P * (tile - 1) : P * tile]
            if tile in GP_WEIGHTS:
                nc.gpsimd.tensor_scalar(
                    out=grouped_weights[tile][:, which],
                    in0=raw.rearrange("p t c -> p c t"),
                    scalar1=1.0,
                    scalar2=0.0,
                    op0=MULT,
                    op1=ADD,
                )
                return
            copy(out=grouped_weights[tile][:, which], in_=raw.rearrange("p t c -> p c t"))

        def quantise_weights(tile):
            nc.vector.quantize_mx(
                out=w_codes[:, tile].rearrange("p w c -> p (w c)").bitcast(FP8X4),
                scales=w_scales[:, tile].rearrange("p w c -> p (w c)"),
                in_=grouped_weights[tile][:].rearrange("p w c t -> p (w c t)"),
            )

        def prepare_weights(tile):
            for which in range(2):
                interleave_weights(tile, which, nc.vector.tensor_copy)
            quantise_weights(tile)

        def project(ft, t):
            ring = ring_of(ft, t)
            pair = []
            for which in range(2):
                acc = next_bank(ring)
                nc.tensor.matmul_mx(
                    out=acc[:],
                    lhsT=w_codes[:, ft, which, :].bitcast(FP8X4),
                    lhsT_scale=w_scales[:, ft, which, :],
                    rhs=x_codes[:, t, :].bitcast(FP8X4),
                    rhs_scale=x_scales[:, t, :],
                    start=True,
                    stop=True,
                )
                pair.append(acc)
            proj_banks[ft, t] = pair

        def finish(ft, t):
            g, half = t // COL_HALVES, t % COL_HALVES
            if half == 0:
                qk_tiles[ft, g] = qk_pool.tile([P, 2, COL_HALVES, TOKENS], BF16, name="qk_bf", align_bytes=64)
            qk_bf = qk_tiles[ft, g]
            q_bank, k_bank = proj_banks[ft, t]
            if ft >= SPLIT_FROM and g in SPLIT_GROUPS:
                if half == 0:
                    q_raw_tiles[ft, g] = raw_pool.tile([P, COL_HALVES, TOKENS], BF16, name="q_raw", align_bytes=64)
                nc.scalar.activation(
                    out=q_raw_tiles[ft, g][:, half, :],
                    in_=q_bank[:],
                    func=ACT.Identity,
                    bias=bias_q_scaled[:, ft : ft + 1],
                    scale=SCALING,
                )
            else:
                nc.vector.scalar_tensor_tensor(
                    out=qk_bf[:, 0, half, :],
                    in0=q_bank[:],
                    scalar=bias_cols[:, ft : ft + 1],
                    in1=keep[:, t, :],
                    op0=ADD,
                    op1=MULT,
                )
            nc.scalar.activation(
                out=qk_bf[:, 1, half, :],
                in_=k_bank[:],
                func=ACT.Identity,
                bias=bias_cols[:, FEATURE_TILES + ft : FEATURE_TILES + ft + 1],
                scale=1.0,
            )

        def make_keep_ones(index):
            g = SPLIT_GROUPS[index]
            nc.scalar.activation(
                out=keep_ones[:, index, :],
                in_=keep[:, COL_HALVES * g : COL_HALVES * g + COL_HALVES, :].rearrange("p h n -> p (h n)"),
                func=ACT.Copy,
                scale=1.0 / SCALING,
            )

        def mask_q(ft, g):
            nc.vector.tensor_tensor(
                out=qk_tiles[ft, g][:, 0].rearrange("p h n -> p (h n)"),
                in0=q_raw_tiles[ft, g][:].rearrange("p h n -> p (h n)"),
                in1=keep_ones[:, SPLIT_GROUPS.index(g), :],
                op=MULT,
            )

        def quantise_qk(ft, g):
            pair, member = g // 2, g % 2
            first, second = sorted_sets[ft % SETS][pair]
            if member == 1 and not (ft == FEATURE_TILES - 1 and g >= ROW_GROUPS - UNSORTED_GROUPS):
                stages_taken[ft, pair] = stages[len(stages_taken) % STAGES]
            target = first if member == 0 else stages_taken.get((ft, pair))
            place = g - (ROW_GROUPS - UNSORTED_GROUPS)
            unsorted = ft == FEATURE_TILES - 1 and place >= 0
            if unsorted:
                target = last_codes[place]
            apart = unsorted and place == UNSORTED_GROUPS - 1
            for which in range(2) if apart else (slice(0, 2),):
                words = slice(COLS * which, COLS * which + COLS) if apart else slice(0, CODE_WORDS)
                bytes_as_words = (
                    slice(CODE_WORDS + COLS // PACK * which, CODE_WORDS + COLS // PACK * (which + 1))
                    if apart
                    else slice(CODE_WORDS, SET_WORDS)
                )
                values = qk_tiles[ft, g][:, which]
                nc.vector.quantize_mx(
                    out=target[:, words].bitcast(FP8X4),
                    scales=target[:, bytes_as_words].bitcast(U8),
                    in_=values.rearrange("p h n -> p (h n)") if apart else values.rearrange("p w h n -> p (w h n)"),
                )
            if unsorted:
                for head in range(2):
                    rows = slice(HALF * head, HALF * head + HALF)
                    (nc.vector if place == UNSORTED_GROUPS - 1 else nc.gpsimd).tensor_copy(
                        out=last_split[place][head][rows, :].bitcast(I32),
                        in_=target[rows, CODE_WORDS : CODE_WORDS + COLS // PACK].bitcast(I32),
                    )
            elif member == 0:
                nc.sync.dma_start(out=second[0:HALF, :].bitcast(I32), in_=first[HALF:P, :].bitcast(I32))
                flush_moves()
            else:
                late_moves.append((first, second, target))
            if unsorted:
                flush_moves()

        def flush_moves():
            while late_moves:
                first, second, stage = late_moves.pop(0)
                nc.sync.dma_start(out=first[HALF:P, :].bitcast(I32), in_=stage[0:HALF, :].bitcast(I32))
                nc.sync.dma_start(out=second[HALF:P, :].bitcast(I32), in_=stage[HALF:P, :].bitcast(I32))

        def logits_pass(ft, i_tile, head, pair, acc):
            codes = sorted_sets[ft % SETS][pair][head]
            scale_words = P // PACK
            nc.tensor.matmul_mx(
                out=acc,
                lhsT=codes[:, P * i_tile : P * i_tile + P].bitcast(FP8X4),
                lhsT_scale=codes[:, CODE_WORDS + scale_words * i_tile : CODE_WORDS + scale_words * (i_tile + 1)].bitcast(U8),
                rhs=codes[:, COLS : 2 * COLS].bitcast(FP8X4),
                rhs_scale=codes[:, CODE_WORDS + COLS // PACK : SET_WORDS].bitcast(U8),
                start=(pair == 0),
                stop=(pair == PAIRS - 1),
            )

        def logits_piece(ft, piece):
            i_tile, head, part = piece // 4, piece // 2 % 2, piece % 2
            if piece % 4 == 0:
                accs[ft, i_tile] = bank(6 + i_tile)
            for pair in range(2 * part, 2 * part + 2):
                logits_pass(ft, i_tile, head, pair, accs[ft, i_tile][:, COLS * head : COLS * head + COLS])

        def tail_passes(kind, index):
            last = FEATURE_TILES - 1
            for n in range(4):
                i_tile, head = n // 2, n % 2
                if kind == "pair":
                    if index == 0:
                        accs[last, n] = bank(4 + n)
                    logits_pass(last, i_tile, head, index, accs[last, n][:, 0:COLS])
                    continue
                codes = last_codes[index]
                if index == 0 and UNSORTED_GROUPS == ROW_GROUPS:
                    accs[last, n] = bank(4 + n)
                nc.tensor.matmul_mx(
                    out=accs[last, n][:, 0:COLS],
                    lhsT=codes[:, P * i_tile : P * i_tile + P].bitcast(FP8X4),
                    lhsT_scale=last_split[index][head][:, P * i_tile : P * i_tile + P],
                    rhs=codes[:, COLS : 2 * COLS].bitcast(FP8X4),
                    rhs_scale=codes[:, CODE_WORDS + COLS // PACK : SET_WORDS].bitcast(U8),
                    start=(index == 0 and UNSORTED_GROUPS == ROW_GROUPS),
                    stop=(index == UNSORTED_GROUPS - 1),
                )

        def store_logits(ft, i_tile):
            result = out_pool.tile([P, 2, COLS], F32, name="result")
            nc.scalar.copy(out=result[:].rearrange("p h j -> p (h j)"), in_=accs[ft, i_tile][:])
            nc.sync.dma_start(
                out=out[2 * ft : 2 * ft + 2, P * i_tile : P * i_tile + P, :].rearrange("h i j -> i h j"),
                in_=result[:],
            )

        warm_bank = psum.tile([P, P], F32, name="warm_bank", tag="bank7")

        def keep_warm(count, out):
            for repeat in range(count):
                nc.tensor.matmul(out=out, lhsT=ident_bf[:], rhs=ident_bf[:], start=True, stop=True)

        keep_warm(WARM_FIRST, warm_bank[:])
        spread_mask(0)
        copy_mask(0, True)
        spread_mask(1)
        copy_mask(1, False)
        spread_mask(2)
        copy_mask(2, True)
        transpose_x(0)
        interleave_weights(0, 0, nc.vector.tensor_copy)
        interleave_weights(0, 1, nc.vector.tensor_copy)
        evacuate_x(0, 0)
        evacuate_x(0, 1)
        quantise_weights(0)
        quantise_x(0)
        spread_mask(3)
        copy_mask(3, True)
        transpose_x(1)
        bias_index = banks_taken[0] % 8
        banks_taken[0] += 1
        bias_bank = psum.tile([P, P], BF16, name="bias_bank", tag="bank%d" % bias_index)
        nc.tensor.transpose(out=bias_bank[:], in_=bias_rows[:], identity=ident_bf[:])
        nc.vector.tensor_copy(out=bias_cols[:], in_=bias_bank[:, 0 : 2 * FEATURE_TILES])
        evacuate_x(1, 0)
        evacuate_x(1, 1)
        nc.vector.tensor_scalar(
            out=bias_q_scaled[:], in0=bias_cols[:, 0:FEATURE_TILES], scalar1=SCALING, scalar2=None, op0=MULT
        )
        project(0, 0)
        finish(0, 0)
        spread_mask(4)
        copy_mask(4, True)
        transpose_x(2)
        quantise_x(1)
        evacuate_x(2, 0)
        evacuate_x(2, 1)
        spread_mask(5)
        copy_mask(5, False)
        order = []
        for t in range(X_UNITS + LAG):
            if t < X_UNITS:
                order.append((0, t))
            if t >= LAG:
                order.append((1, t - LAG))
        order += [(ft, t) for ft in (2, 3) for t in range(X_UNITS)]

        pieces = []
        tail_pairs = []
        to_mask = []
        to_quantise = []
        for slot, (ft, t) in enumerate(order):
            streaming = ft == 0
            if streaming and t + PREP_AHEAD < X_UNITS:
                transpose_x(t + PREP_AHEAD)
            if streaming and t + HEAD_MASKS < X_UNITS:
                spread_mask(t + HEAD_MASKS)
            if slot < 2 * X_UNITS:
                if slot > 0:
                    finish(ft, t)
                if streaming and t + 2 < X_UNITS:
                    quantise_x(t + 2)
            if slot + 1 < 2 * X_UNITS:
                project(*order[slot + 1])
            stores = []
            if pieces and slot >= pieces[0][0]:
                for repeat in range(1 if ft < FEATURE_TILES - 1 else 2):
                    if pieces:
                        ready, lft, piece = pieces.pop(0)
                        logits_piece(lft, piece)
                        if piece % 4 == 3:
                            stores.append((lft, piece // 4))
            elif not pieces and tail_pairs and slot >= tail_pairs[0][0]:
                tail_passes(*tail_pairs.pop(0)[1:])
            if 2 * X_UNITS <= slot + 1 < len(order):
                project(*order[slot + 1])
            if slot >= 2 * X_UNITS:
                finish(ft, t)
            while to_mask and to_mask[0][0] <= slot:
                when, mft, g = to_mask.pop(0)
                mask_q(mft, g)
            while to_quantise and to_quantise[0][0] <= slot:
                when, qft, g = to_quantise.pop(0)
                quantise_qk(qft, g)
                if qft == FEATURE_TILES - 1:
                    if g >= ROW_GROUPS - UNSORTED_GROUPS:
                        tail_pairs.append((slot + 2, "group", g - (ROW_GROUPS - UNSORTED_GROUPS)))
                    elif g % 2 == 1:
                        tail_pairs.append((slot + SORT_LAG, "pair", g // 2))
                elif g == ROW_GROUPS - 1:
                    for piece in range(8):
                        pieces.append((slot + SORT_LAG, qft, piece))
            if t % COL_HALVES == COL_HALVES - 1:
                g = t // COL_HALVES
                if ft >= SPLIT_FROM and g in SPLIT_GROUPS:
                    to_mask.append((slot + 1, ft, g))
                    to_quantise.append((slot + 1 + 1, ft, g))
                else:
                    to_quantise.append((slot + 1, ft, g))
            if streaming and t + PREP_AHEAD < X_UNITS:
                evacuate_x(t + PREP_AHEAD, 0)
                evacuate_x(t + PREP_AHEAD, 1)
            if streaming and t + HEAD_MASKS < X_UNITS:
                copy_mask(t + HEAD_MASKS, t + HEAD_MASKS in MASK_SCALAR)
            for first, first_slot, second_slot, quantise_slot, which_engine in W_STEPS:
                copy = {"v": nc.vector.tensor_copy, "s": nc.scalar.copy}[which_engine]
                if slot == first_slot:
                    interleave_weights(first, 0, copy)
                if slot == second_slot:
                    interleave_weights(first, 1, copy)
                if slot == quantise_slot:
                    quantise_weights(first)
            if ONES_SLOT <= slot < ONES_SLOT + len(SPLIT_GROUPS):
                make_keep_ones(slot - ONES_SLOT)
            for item in stores:
                store_logits(*item)

        quantise_qk(FEATURE_TILES - 1, ROW_GROUPS - 1)
        last = FEATURE_TILES - 1
        tail_pairs.append((0, "group", UNSORTED_GROUPS - 1))
        for item in tail_pairs:
            tail_passes(*item[1:])
        for n in range(4):
            i_tile, head = n // 2, n % 2
            result = out_pool.tile([P, COLS], F32, name="last_result_%d" % head)
            if head == 0:
                nc.scalar.copy(out=result[:], in_=accs[last, n][:, 0:COLS])
            else:
                nc.vector.tensor_copy(out=result[:], in_=accs[last, n][:, 0:COLS])
            nc.sync.dma_start(out=out[2 * last + head, P * i_tile : P * i_tile + P, :], in_=result[:])
